import numpy as np
import ml_dtypes


def mxq(x, axis, fmt="e4m3"):
    dtype, down = {"e4m3": (ml_dtypes.float8_e4m3fn, 7), "e5m2": (ml_dtypes.float8_e5m2, 14)}[fmt]
    v = np.moveaxis(np.asarray(x, np.float32).astype(ml_dtypes.bfloat16).astype(np.float64), axis, -1)
    blocks = v.reshape(v.shape[:-1] + (-1, 32))
    amax = np.abs(blocks).max(-1, keepdims=True)
    byte = np.maximum(np.where(amax > 0, np.frexp(amax)[1] - 1 + 127, 0) - down, 1)
    scale = np.exp2(byte - 127.0)
    codes = (blocks / scale).astype(np.float32).astype(dtype).astype(np.float64)
    return np.moveaxis((codes * scale).reshape(v.shape), -1, axis)


WIDE = False


def mx_kscale(k):
    if not WIDE:
        return np.ones(k)
    levels = np.array([10, -10, 5, -5, 0])
    a = np.random.permutation(np.resize(levels, k // 512 * 4)).reshape(k // 512, 4)
    idx = np.arange(k)
    return np.exp2(a[idx // 512, idx % 128 // 32])


BF16 = ml_dtypes.bfloat16


def bf(x):
    return np.asarray(x, np.float32).astype(BF16)


def f64(x):
    return np.asarray(x).astype(np.float64)


E2M1 = np.array([0.0, 0.5, 1.0, 1.5, 2.0, 3.0, 4.0, 6.0, -0.0, -0.5, -1.0, -1.5, -2.0, -3.0, -4.0, -6.0])


def pack_weight(w, fmt):
    k, n = w.shape
    w = f64(bf(w)).reshape(k // 32, 32, n)
    amax = np.abs(w).max(1)
    if fmt == "e4m3":
        byte = np.frexp(amax)[1] - 1 + 127 - 7
    else:
        mant, ex = np.frexp(amax / 6.0)
        byte = np.where(mant > 0.5, ex, ex - 1) + 127
    byte = np.clip(np.where(amax > 0, byte, 1), 1, 254)
    scaled = (w * np.exp2(127.0 - byte)[:, None, :]).reshape(k, n).astype(np.float32)
    by_word = np.ascontiguousarray(scaled.reshape(k // 512, 128, 4, n).transpose(0, 1, 3, 2))
    if fmt == "e4m3":
        words = by_word.astype(ml_dtypes.float8_e4m3fn).view(np.uint8)
    else:
        c = by_word.astype(ml_dtypes.float4_e2m1fn).view(np.uint8) & 0xF
        words = c[..., 0::2] | (c[..., 1::2] << 4)
    return np.ascontiguousarray(words), np.ascontiguousarray(byte.astype(np.uint8).reshape(k // 512, 16, n))


def unpack_weight(words, scales, fmt):
    g, p, n, _ = words.shape
    if fmt == "e4m3":
        vals = np.ascontiguousarray(words).view(ml_dtypes.float8_e4m3fn).astype(np.float64)
    else:
        nib = np.empty((g, p, n, 4), np.uint8)
        nib[..., 0::2] = words & 0xF
        nib[..., 1::2] = words >> 4
        vals = E2M1[nib]
    vals = vals * np.repeat(np.exp2(scales.astype(np.float64) - 127.0), 8, axis=1)[..., None]
    return vals.transpose(0, 1, 3, 2).reshape(g * 512, n)


B, N, C, DIM, H = 4, 128, 2048, 2048, 16
D = DIM // H // 2
LAYER_NUM = 12
LAM_INIT = 0.8 - 0.6 * np.exp(-0.3 * LAYER_NUM)
SCALE = D ** -0.5
FMT = "e4m3"


def split_qk(y):
    y = y.reshape(B, N, H, D, 2)
    return np.moveaxis(y, -1, 2).reshape(B, N, 2 * H, D)


def setup_inputs():
    s = mx_kscale(C)
    ls = 0.45 / D ** 0.25
    x = bf(np.random.standard_normal((B, N, C)) * s)
    Wq = np.random.standard_normal((DIM, C)) / np.sqrt(C) / s
    Wk = np.random.standard_normal((DIM, C)) / np.sqrt(C) / s
    Wq_words, Wq_scales = pack_weight(np.ascontiguousarray(Wq.T), FMT)
    Wk_words, Wk_scales = pack_weight(np.ascontiguousarray(Wk.T), FMT)
    return {"x": x,
            "Wq_words": Wq_words,
            "Wq_scales": Wq_scales,
            "Wk_words": Wk_words,
            "Wk_scales": Wk_scales,
            "lq1": bf(np.random.standard_normal(D) * ls),
            "lq2": bf(np.random.standard_normal(D) * ls),
            "lk1": bf(np.random.standard_normal(D) * ls),
            "lk2": bf(np.random.standard_normal(D) * ls)}


def reference(x, Wq_words, Wq_scales, Wk_words, Wk_scales, lq1, lq2, lk1, lk2):
    xq = mxq(f64(x), 2, "e4m3")
    q = split_qk(xq @ unpack_weight(Wq_words, Wq_scales, FMT)) * SCALE
    k = split_qk(xq @ unpack_weight(Wk_words, Wk_scales, FMT))
    sc = np.stack([(q[:, :, i:i + 1, :] * k).sum(-1) for i in range(2 * H)], axis=2)
    e = np.exp(sc - sc.max(-1, keepdims=True))
    att = e / e.sum(-1, keepdims=True)
    lam = np.exp(np.sum(f64(lq1) * f64(lk1))) - np.exp(np.sum(f64(lq2) * f64(lk2))) + LAM_INIT
    return att[:, :, :H, :H] - lam * att[:, :, H:, H:]

@@ -1,0 +1,283 @@
+from contextlib import ExitStack
+
+import math
+
+import concourse.masks as masks
+import concourse.mybir as mybir
+
+F32 = mybir.dt.float32
+BF16 = mybir.dt.bfloat16
+I32 = mybir.dt.int32
+U8 = mybir.dt.uint8
+U32 = mybir.dt.uint32
+FP8X4 = mybir.dt.float8_e4m3fn_x4
+ALU = mybir.AluOpType
+ACT = mybir.ActivationFunctionType
+AXIS = mybir.AxisListType
+
+P = 128
+TILES = 4
+C = 2048
+K_PASS = 512
+PASSES = C // K_PASS
+CHUNK = 512
+CHUNKS = 2048 // CHUNK
+H = 16
+D = 64
+ROWS = 2 * H
+CHUNK_HEADS = CHUNK // (2 * D)
+BANK = 512
+BATCH = 16
+BANK_N = BANK // (2 * ROWS)
+
+SCALE = D ** -0.5
+LAM_INIT = 0.8 - 0.6 * math.exp(-0.3 * 12)
+
+FLOPS = 2 * TILES * P * C * 2 * 2048 + 2 * TILES * P * ROWS * ROWS * D
+
+
+def tile_differentialattention_pa_kernel(
+    tc, x, Wq_words, Wq_scales, Wk_words, Wk_scales, lq1, lq2, lk1, lk2, out
+):
+    nc = tc.nc
+    with ExitStack() as ctx:
+        keep = ctx.enter_context(tc.tile_pool(name="keep", bufs=1))
+        x_pool = ctx.enter_context(tc.tile_pool(name="x_pool", bufs=2))
+        w_pool = ctx.enter_context(tc.tile_pool(name="w_pool", bufs=4))
+        y_pool = ctx.enter_context(tc.tile_pool(name="y_pool", bufs=2))
+        soft = ctx.enter_context(tc.tile_pool(name="soft", bufs=3))
+        psum = ctx.enter_context(tc.psum_pool(name="psum", bufs=8))
+        ctx.enter_context(tc.manual_schedule())
+
+        x_sb = []
+        for t in range(TILES):
+            x_tile = keep.tile([P, C], BF16, name="x_sb%d" % t)
+            nc.sync.dma_start(out=x_tile[:], in_=x[t])
+            x_sb.append(x_tile)
+
+        lam_vecs = keep.tile([P, 4, D], BF16)
+        for v, vec in enumerate((lq1, lq2, lk1, lk2)):
+            nc.scalar.dma_start(out=lam_vecs[:, v, :], in_=vec.partition_broadcast(P))
+
+        w_planes = []
+        for name, scales in (("q", Wq_scales), ("k", Wk_scales)):
+            planes = keep.tile([P, 2048], U8, name="w_planes_" + name, align_bytes=64)
+            nc.vector.memset(planes[:].bitcast(I32), 0)
+            for quad in range(4):
+                nc.sync.dma_start(
+                    out=planes[32 * quad : 32 * quad + 16, :].bitcast(I32),
+                    in_=scales[:, 4 * quad : 4 * quad + 4, :].bitcast(I32),
+                )
+            w_planes.append(planes)
+
+        def load_chunk(c):
+            words = (Wq_words, Wk_words)[c % 2]
+            first = 4 * CHUNK * (c // 2)
+            w = w_pool.tile([P, PASSES, 4 * CHUNK], U8, tag="w", align_bytes=64)
+            nc.sync.dma_start(
+                out=w[:].bitcast(I32),
+                in_=words.rearrange("g p n t -> p g (n t)")[:, :, first : first + 4 * CHUNK].bitcast(I32),
+            )
+            return w
+
+        chunk_words = [load_chunk(c) for c in range(4)]
+
+        ident = keep.tile([P, P], F32)
+        masks.make_identity(nc, ident[:])
+
+        x_codes = keep.tile([P, TILES, PASSES * P], U32, align_bytes=64)
+        x_planes = keep.tile([P, TILES, PASSES * P], U8, align_bytes=64)
+        for t in range(TILES):
+            words = x_sb[t][:].bitcast(F32)
+            grouped = x_pool.tile([P, PASSES * P * 4], BF16, tag="grouped", align_bytes=64)
+            grouped_words = grouped[:].bitcast(F32).rearrange("p (g n u) -> p g n u", g=PASSES, u=2)
+            for half in range(2):
+                bank = psum.tile([P, BANK], F32, tag="bank")
+                planes = bank[:].rearrange("p (g u n) -> p g u n", g=2, u=2)
+                for gg in range(2):
+                    g = 2 * half + gg
+                    for u in range(2):
+                        nc.tensor.transpose(
+                            planes[:, gg, u, :], words[:, 256 * g + u : 256 * (g + 1) : 2], ident[:]
+                        )
+                copy = (nc.vector.tensor_copy, nc.scalar.copy)[half]
+                copy(
+                    out=grouped_words[:, 2 * half : 2 * half + 2, :, :],
+                    in_=planes.rearrange("p g u n -> p g n u"),
+                )
+            nc.vector.quantize_mx(
+                out=x_codes[:, t, :].bitcast(FP8X4), scales=x_planes[:, t, :], in_=grouped[:]
+            )
+
+        ident_tja = ident[:].rearrange("q (t j a) -> q t j a", j=2, a=H)
+        row_is = keep.tile([P, 2], F32)
+        for j in range(2):
+            nc.vector.tensor_reduce(out=row_is[:, j : j + 1], in_=ident_tja[:, :, j, :], axis=AXIS.XY, op=ALU.add)
+        q_mask = keep.tile([P, 2], F32)
+        nc.vector.tensor_reduce(
+            out=q_mask[:], in_=ident[:].rearrange("q (s d) -> q s d", s=2), axis=AXIS.X, op=ALU.add
+        )
+        nc.vector.tensor_scalar_mul(out=q_mask[:], in0=q_mask[:], scalar1=SCALE)
+        lam_prod = keep.tile([P, 2, D], F32)
+        nc.vector.tensor_tensor(out=lam_prod[:], in0=lam_vecs[:, 0:2, :], in1=lam_vecs[:, 2:4, :], op=ALU.mult)
+        lam_dots = keep.tile([P, 2], F32)
+        nc.vector.tensor_reduce(out=lam_dots[:], in_=lam_prod[:], axis=AXIS.X, op=ALU.add)
+        lam_exps = keep.tile([P, 2], F32)
+        nc.scalar.activation(out=lam_exps[:], in_=lam_dots[:], func=ACT.Exp)
+
+        q_t = keep.tile([P, P, TILES * ROWS], F32)
+        k_t = keep.tile([P, P, 2 * ROWS], F32)
+
+        def project(c):
+            w = chunk_words[c]
+            planes = w_planes[c % 2]
+            cols = slice(CHUNK * (c // 2), CHUNK * (c // 2 + 1))
+            y = y_pool.tile([P, 2, 2, CHUNK_HEADS, 2 * D], F32, tag="y")
+            for t in range(TILES):
+                acc = psum.tile([P, BANK], F32, tag="bank")
+                for g in range(PASSES):
+                    nc.tensor.matmul_mx(
+                        out=acc[:],
+                        lhsT=x_codes[:, t, P * g : P * (g + 1)].bitcast(FP8X4),
+                        lhsT_scale=x_planes[:, t, P * g : P * (g + 1)],
+                        rhs=w[:, g, :].bitcast(FP8X4),
+                        rhs_scale=planes[4 * g : P, cols],
+                        start=(g == 0),
+                        stop=(g == PASSES - 1),
+                    )
+                copy = (nc.vector.tensor_copy, nc.scalar.copy)[t % 2]
+                copy(
+                    out=y[:, t // 2, :, :, D * (t % 2) : D * (t % 2 + 1)],
+                    in_=acc[:].rearrange("p (h d j) -> p j h d", d=D, j=2),
+                )
+            return y
+
+        def transpose_chunk(c, y):
+            for pair in range(2):
+                for j in range(2):
+                    bank = psum.tile([P, BANK], F32, tag="bank")
+                    by_head = bank[:].rearrange("k (h n) -> k h n", h=CHUNK_HEADS)
+                    for h in range(CHUNK_HEADS):
+                        nc.tensor.transpose(by_head[:, h, :], y[:, pair, j, h, :], ident[:])
+                    by_n = by_head.rearrange("k h n -> k n h")
+                    row = H * j + CHUNK_HEADS * (c // 2)
+                    if c % 2 == 1:
+                        copy = (nc.vector.tensor_copy, nc.scalar.copy)[j]
+                        first = ROWS * pair + row
+                        copy(out=k_t[:, :, first : first + CHUNK_HEADS], in_=by_n)
+                    else:
+                        for s in range(2):
+                            first = ROWS * (2 * pair + s) + row
+                            dst = q_t[:, :, first : first + CHUNK_HEADS]
+                            if j == 0:
+                                nc.vector.tensor_scalar_mul(out=dst, in0=by_n, scalar1=q_mask[:, s : s + 1])
+                            else:
+                                nc.scalar.activation(out=dst, in_=by_n, func=ACT.Copy, scale=q_mask[:, s : s + 1])
+
+        n_chunks = 2 * CHUNKS
+        y_tiles = [project(0)]
+        for c in range(1, n_chunks):
+            if c + 3 < n_chunks:
+                chunk_words.append(load_chunk(c + 3))
+            y_tiles.append(project(c))
+            transpose_chunk(c - 1, y_tiles[c - 1])
+        transpose_chunk(n_chunks - 1, y_tiles[n_chunks - 1])
+
+        neg_lam = keep.tile([P, 1], F32)
+        nc.vector.tensor_tensor(out=neg_lam[:], in0=lam_exps[:, 1:2], in1=lam_exps[:, 0:1], op=ALU.subtract)
+        nc.vector.tensor_scalar_add(out=neg_lam[:], in0=neg_lam[:], scalar1=-LAM_INIT)
+        combine = keep.tile([P, TILES, H], F32)
+        nc.vector.scalar_tensor_tensor(
+            out=combine[:],
+            in0=ident_tja[:, :, 1, :],
+            scalar=neg_lam[:, 0:1],
+            in1=ident_tja[:, :, 0, :],
+            op0=ALU.mult,
+            op1=ALU.add,
+        )
+
+        weights = keep.tile([P, H, P], F32)
+
+        def scores(b):
+            e = soft.tile([P, BATCH, ROWS], F32, tag="e")
+            for part in range(BATCH // BANK_N):
+                bank = psum.tile([P, BANK], F32, tag="bank")
+                sc = bank[:].rearrange("q (n a m) -> q n a m", a=2, m=ROWS)
+                for i in range(BANK_N):
+                    n = BATCH * b + BANK_N * part + i
+                    nc.tensor.matmul(
+                        out=bank[:, 2 * ROWS * i : 2 * ROWS * (i + 1)],
+                        lhsT=q_t[:, n, :],
+                        rhs=k_t[:, n, :],
+                        start=True,
+                        stop=True,
+                    )
+                for pair in range(2):
+                    rows = slice(64 * pair, 64 * (pair + 1))
+                    nc.scalar.copy(out=e[rows, BANK_N * part : BANK_N * (part + 1), :], in_=sc[rows, :, pair, :])
+            return e
+
+        def subtract_max(e):
+            top = soft.tile([P, BATCH], F32, tag="top")
+            nc.vector.tensor_reduce(out=top[:], in_=e[:], axis=AXIS.X, op=ALU.max)
+            nc.vector.tensor_tensor(
+                out=e[:], in0=e[:], in1=top[:].unsqueeze(2).to_broadcast([P, BATCH, ROWS]), op=ALU.subtract
+            )
+
+        def pick_odd(e):
+            odd = soft.tile([P, BATCH, H], F32, tag="odd")
+            nc.scalar.activation(out=odd[:], in_=e[:, :, H:ROWS], func=ACT.Copy, scale=row_is[:, 1:2])
+            return odd
+
+        def normalise(b, e, odd):
+            total = soft.tile([P, BATCH], F32, tag="total")
+            nc.vector.tensor_reduce(out=total[:], in_=e[:], axis=AXIS.X, op=ALU.add)
+            inverse = soft.tile([P, BATCH], F32, tag="inverse")
+            nc.vector.reciprocal(out=inverse[:], in_=total[:])
+            picked = soft.tile([P, BATCH, H], F32, tag="picked")
+            nc.vector.scalar_tensor_tensor(
+                out=picked[:], in0=e[:, :, 0:H], scalar=row_is[:, 0:1], in1=odd[:], op0=ALU.mult, op1=ALU.add
+            )
+            nc.vector.tensor_tensor(
+                out=weights[:, :, BATCH * b : BATCH * (b + 1)],
+                in0=picked[:].rearrange("q n h -> q h n"),
+                in1=inverse[:].unsqueeze(1).to_broadcast([P, H, BATCH]),
+                op=ALU.mult,
+            )
+
+        batches = P // BATCH
+        previous = None
+        for b in range(batches + 1):
+            if b < batches:
+                e = scores(b)
+            if previous is not None:
+                odd = pick_odd(previous)
+            if b < batches:
+                subtract_max(e)
+                nc.scalar.activation(out=e[:], in_=e[:], func=ACT.Exp)
+            if previous is not None:
+                normalise(b - 1, previous, odd)
+            previous = e
+
+        result = keep.tile([P, TILES * H, H], F32)
+        heads_per_bank = BANK // (TILES * H)
+        for part in range(H // heads_per_bank):
+            bank = psum.tile([P, BANK], F32, tag="bank")
+            by_h = bank[:].rearrange("n (h c) -> n h c", h=heads_per_bank)
+            for i in range(heads_per_bank):
+                nc.tensor.matmul(
+                    out=by_h[:, i, :],
+                    lhsT=weights[:, heads_per_bank * part + i, :],
+                    rhs=combine[:].rearrange("q t a -> q (t a)"),
+                    start=True,
+                    stop=True,
+                )
+            copy = (nc.vector.tensor_copy, nc.scalar.copy)[part]
+            copy(
+                out=result[:, :, heads_per_bank * part : heads_per_bank * (part + 1)],
+                in_=by_h.rearrange("n h c -> n c h"),
+            )
+        nc.sync.dma_start(
+            out=out.rearrange("b n a h -> n b (a h)"),
+            in_=result[:].rearrange("n (t a) h -> n t (a h)", t=TILES),
+        )

@@ -59,8 +59,7 @@ def tile_differentialattention_pa_kernel(
         for v, vec in enumerate((lq1, lq2, lk1, lk2)):
             nc.scalar.dma_start(out=lam_vecs[:, v, :], in_=vec.partition_broadcast(P))
 
-        w_planes = []
-        for name, scales in (("q", Wq_scales), ("k", Wk_scales)):
+        def load_planes(name, scales):
             planes = keep.tile([P, 2048], U8, name="w_planes_" + name, align_bytes=64)
             nc.vector.memset(planes[:].bitcast(I32), 0)
             for quad in range(4):
@@ -68,7 +67,7 @@ def tile_differentialattention_pa_kernel(
                     out=planes[32 * quad : 32 * quad + 16, :].bitcast(I32),
                     in_=scales[:, 4 * quad : 4 * quad + 4, :].bitcast(I32),
                 )
-            w_planes.append(planes)
+            return planes
 
         def load_chunk(c):
             words = (Wq_words, Wk_words)[c % 2]
@@ -80,7 +79,12 @@ def tile_differentialattention_pa_kernel(
             )
             return w
 
-        chunk_words = [load_chunk(c) for c in range(4)]
+        q_planes = load_planes("q", Wq_scales)
+        chunk_words = [load_chunk(0)]
+        k_planes = load_planes("k", Wk_scales)
+        w_planes = (q_planes, k_planes)
+        for c in range(1, 4):
+            chunk_words.append(load_chunk(c))
 
         ident = keep.tile([P, P], F32)
         masks.make_identity(nc, ident[:])
@@ -246,18 +250,18 @@ def tile_differentialattention_pa_kernel(
             )
 
         batches = P // BATCH
-        previous = None
-        for b in range(batches + 1):
+        e_tiles = []
+        odd_tiles = []
+        for b in range(batches + 2):
             if b < batches:
-                e = scores(b)
-            if previous is not None:
-                odd = pick_odd(previous)
-            if b < batches:
+                e_tiles.append(scores(b))
+            if 1 <= b <= batches:
+                e = e_tiles[b - 1]
                 subtract_max(e)
                 nc.scalar.activation(out=e[:], in_=e[:], func=ACT.Exp)
-            if previous is not None:
-                normalise(b - 1, previous, odd)
-            previous = e
+                odd_tiles.append(pick_odd(e))
+            if b >= 2:
+                normalise(b - 2, e_tiles[b - 2], odd_tiles[b - 2])
 
         result = keep.tile([P, TILES * H, H], F32)
         heads_per_bank = BANK // (TILES * H)

@@ -27,6 +27,7 @@ D = 64
 ROWS = 2 * H
 CHUNK_HEADS = CHUNK // (2 * D)
 BANK = 512
+CHUNK_ROWS = 2 * CHUNK_HEADS
 BATCH = 16
 BANK_N = BANK // (2 * ROWS)
 
@@ -88,6 +89,8 @@ def tile_differentialattention_pa_kernel(
 
         ident = keep.tile([P, P], F32)
         masks.make_identity(nc, ident[:])
+        ident_bf = keep.tile([P, P], BF16)
+        masks.make_identity(nc, ident_bf[:])
 
         x_codes = keep.tile([P, TILES, PASSES * P], U32, align_bytes=64)
         x_planes = keep.tile([P, TILES, PASSES * P], U8, align_bytes=64)
@@ -113,10 +116,10 @@ def tile_differentialattention_pa_kernel(
                 out=x_codes[:, t, :].bitcast(FP8X4), scales=x_planes[:, t, :], in_=grouped[:]
             )
 
-        ident_tja = ident[:].rearrange("q (t j a) -> q t j a", j=2, a=H)
+        ident_gjx = ident[:].rearrange("q (g j x) -> q g j x", j=2, x=CHUNK_HEADS)
         row_is = keep.tile([P, 2], F32)
         for j in range(2):
-            nc.vector.tensor_reduce(out=row_is[:, j : j + 1], in_=ident_tja[:, :, j, :], axis=AXIS.XY, op=ALU.add)
+            nc.vector.tensor_reduce(out=row_is[:, j : j + 1], in_=ident_gjx[:, :, j, :], axis=AXIS.XY, op=ALU.add)
         q_mask = keep.tile([P, 2], F32)
         nc.vector.tensor_reduce(
             out=q_mask[:], in_=ident[:].rearrange("q (s d) -> q s d", s=2), axis=AXIS.X, op=ALU.add
@@ -129,14 +132,14 @@ def tile_differentialattention_pa_kernel(
         lam_exps = keep.tile([P, 2], F32)
         nc.scalar.activation(out=lam_exps[:], in_=lam_dots[:], func=ACT.Exp)
 
-        q_t = keep.tile([P, P, TILES * ROWS], F32)
-        k_t = keep.tile([P, P, 2 * ROWS], F32)
+        q_parts = [keep.tile([P, P, TILES * ROWS], BF16, name="q_" + part) for part in ("hi", "lo")]
+        k_parts = [keep.tile([P, P, 2 * ROWS], BF16, name="k_" + part) for part in ("hi", "lo")]
 
         def project(c):
             w = chunk_words[c]
             planes = w_planes[c % 2]
             cols = slice(CHUNK * (c // 2), CHUNK * (c // 2 + 1))
-            y = y_pool.tile([P, 2, 2, CHUNK_HEADS, 2 * D], F32, tag="y")
+            y = y_pool.tile([P, 2, 2, 2, CHUNK_HEADS, 2 * D], BF16, tag="y")
             for t in range(TILES):
                 acc = psum.tile([P, BANK], F32, tag="bank")
                 for g in range(PASSES):
@@ -149,31 +152,33 @@ def tile_differentialattention_pa_kernel(
                         start=(g == 0),
                         stop=(g == PASSES - 1),
                     )
-                copy = (nc.vector.tensor_copy, nc.scalar.copy)[t % 2]
-                copy(
-                    out=y[:, t // 2, :, :, D * (t % 2) : D * (t % 2 + 1)],
-                    in_=acc[:].rearrange("p (h d j) -> p j h d", d=D, j=2),
-                )
+                by_row = acc[:].rearrange("p (h d j) -> p j h d", d=D, j=2)
+                side = slice(D * (t % 2), D * (t % 2 + 1))
+                hi = y[:, 0, t // 2, :, :, side]
+                lo = y[:, 1, t // 2, :, :, side]
+                nc.scalar.copy(out=hi, in_=by_row)
+                nc.vector.tensor_tensor(out=lo, in0=by_row, in1=hi, op=ALU.subtract)
             return y
 
         def transpose_chunk(c, y):
-            for pair in range(2):
-                for j in range(2):
-                    bank = psum.tile([P, BANK], F32, tag="bank")
-                    by_head = bank[:].rearrange("k (h n) -> k h n", h=CHUNK_HEADS)
-                    for h in range(CHUNK_HEADS):
-                        nc.tensor.transpose(by_head[:, h, :], y[:, pair, j, h, :], ident[:])
-                    by_n = by_head.rearrange("k h n -> k n h")
-                    row = H * j + CHUNK_HEADS * (c // 2)
+            row = CHUNK_ROWS * (c // 2)
+            for part in range(2):
+                for pair in range(2):
+                    bank = psum.tile([P, 2 * BANK], BF16, tag="bank")
+                    by_row = bank[:].rearrange("k (j h n) -> k j h n", j=2, h=CHUNK_HEADS)
+                    for j in range(2):
+                        for h in range(CHUNK_HEADS):
+                            nc.tensor.transpose(by_row[:, j, h, :], y[:, part, pair, j, h, :], ident_bf[:])
+                    by_n = bank[:].rearrange("k (r n) -> k n r", r=CHUNK_ROWS)
                     if c % 2 == 1:
-                        copy = (nc.vector.tensor_copy, nc.scalar.copy)[j]
+                        copy = (nc.vector.tensor_copy, nc.scalar.copy)[pair]
                         first = ROWS * pair + row
-                        copy(out=k_t[:, :, first : first + CHUNK_HEADS], in_=by_n)
+                        copy(out=k_parts[part][:, :, first : first + CHUNK_ROWS], in_=by_n)
                     else:
                         for s in range(2):
                             first = ROWS * (2 * pair + s) + row
-                            dst = q_t[:, :, first : first + CHUNK_HEADS]
-                            if j == 0:
+                            dst = q_parts[part][:, :, first : first + CHUNK_ROWS]
+                            if pair == 0:
                                 nc.vector.tensor_scalar_mul(out=dst, in0=by_n, scalar1=q_mask[:, s : s + 1])
                             else:
                                 nc.scalar.activation(out=dst, in_=by_n, func=ACT.Copy, scale=q_mask[:, s : s + 1])
@@ -190,17 +195,12 @@ def tile_differentialattention_pa_kernel(
         neg_lam = keep.tile([P, 1], F32)
         nc.vector.tensor_tensor(out=neg_lam[:], in0=lam_exps[:, 1:2], in1=lam_exps[:, 0:1], op=ALU.subtract)
         nc.vector.tensor_scalar_add(out=neg_lam[:], in0=neg_lam[:], scalar1=-LAM_INIT)
-        combine = keep.tile([P, TILES, H], F32)
+        coef = keep.tile([P, 1], F32)
         nc.vector.scalar_tensor_tensor(
-            out=combine[:],
-            in0=ident_tja[:, :, 1, :],
-            scalar=neg_lam[:, 0:1],
-            in1=ident_tja[:, :, 0, :],
-            op0=ALU.mult,
-            op1=ALU.add,
+            out=coef[:], in0=row_is[:, 1:2], scalar=neg_lam[:, 0:1], in1=row_is[:, 0:1], op0=ALU.mult, op1=ALU.add
         )
 
-        weights = keep.tile([P, H, P], F32)
+        weights = keep.tile([P, ROWS, P], F32)
 
         def scores(b):
             e = soft.tile([P, BATCH, ROWS], F32, tag="e")
@@ -209,13 +209,15 @@ def tile_differentialattention_pa_kernel(
                 sc = bank[:].rearrange("q (n a m) -> q n a m", a=2, m=ROWS)
                 for i in range(BANK_N):
                     n = BATCH * b + BANK_N * part + i
-                    nc.tensor.matmul(
-                        out=bank[:, 2 * ROWS * i : 2 * ROWS * (i + 1)],
-                        lhsT=q_t[:, n, :],
-                        rhs=k_t[:, n, :],
-                        start=True,
-                        stop=True,
-                    )
+                    terms = ((0, 0), (0, 1), (1, 0))
+                    for term, (q_part, k_part) in enumerate(terms):
+                        nc.tensor.matmul(
+                            out=bank[:, 2 * ROWS * i : 2 * ROWS * (i + 1)],
+                            lhsT=q_parts[q_part][:, n, :],
+                            rhs=k_parts[k_part][:, n, :],
+                            start=(term == 0),
+                            stop=(term == len(terms) - 1),
+                        )
                 for pair in range(2):
                     rows = slice(64 * pair, 64 * (pair + 1))
                     nc.scalar.copy(out=e[rows, BANK_N * part : BANK_N * (part + 1), :], in_=sc[rows, :, pair, :])
@@ -228,30 +230,21 @@ def tile_differentialattention_pa_kernel(
                 out=e[:], in0=e[:], in1=top[:].unsqueeze(2).to_broadcast([P, BATCH, ROWS]), op=ALU.subtract
             )
 
-        def pick_odd(e):
-            odd = soft.tile([P, BATCH, H], F32, tag="odd")
-            nc.scalar.activation(out=odd[:], in_=e[:, :, H:ROWS], func=ACT.Copy, scale=row_is[:, 1:2])
-            return odd
-
-        def normalise(b, e, odd):
+        def normalise(b, e):
             total = soft.tile([P, BATCH], F32, tag="total")
             nc.vector.tensor_reduce(out=total[:], in_=e[:], axis=AXIS.X, op=ALU.add)
             inverse = soft.tile([P, BATCH], F32, tag="inverse")
             nc.vector.reciprocal(out=inverse[:], in_=total[:])
-            picked = soft.tile([P, BATCH, H], F32, tag="picked")
-            nc.vector.scalar_tensor_tensor(
-                out=picked[:], in0=e[:, :, 0:H], scalar=row_is[:, 0:1], in1=odd[:], op0=ALU.mult, op1=ALU.add
-            )
+            nc.vector.tensor_scalar_mul(out=inverse[:], in0=inverse[:], scalar1=coef[:, 0:1])
             nc.vector.tensor_tensor(
                 out=weights[:, :, BATCH * b : BATCH * (b + 1)],
-                in0=picked[:].rearrange("q n h -> q h n"),
-                in1=inverse[:].unsqueeze(1).to_broadcast([P, H, BATCH]),
+                in0=e[:].rearrange("q n m -> q m n"),
+                in1=inverse[:].unsqueeze(1).to_broadcast([P, ROWS, BATCH]),
                 op=ALU.mult,
             )
 
         batches = P // BATCH
         e_tiles = []
-        odd_tiles = []
         for b in range(batches + 2):
             if b < batches:
                 e_tiles.append(scores(b))
@@ -259,29 +252,24 @@ def tile_differentialattention_pa_kernel(
                 e = e_tiles[b - 1]
                 subtract_max(e)
                 nc.scalar.activation(out=e[:], in_=e[:], func=ACT.Exp)
-                odd_tiles.append(pick_odd(e))
             if b >= 2:
-                normalise(b - 2, e_tiles[b - 2], odd_tiles[b - 2])
+                normalise(b - 2, e_tiles[b - 2])
 
-        result = keep.tile([P, TILES * H, H], F32)
-        heads_per_bank = BANK // (TILES * H)
-        for part in range(H // heads_per_bank):
-            bank = psum.tile([P, BANK], F32, tag="bank")
-            by_h = bank[:].rearrange("n (h c) -> n h c", h=heads_per_bank)
-            for i in range(heads_per_bank):
-                nc.tensor.matmul(
-                    out=by_h[:, i, :],
-                    lhsT=weights[:, heads_per_bank * part + i, :],
-                    rhs=combine[:].rearrange("q t a -> q (t a)"),
-                    start=True,
-                    stop=True,
-                )
-            copy = (nc.vector.tensor_copy, nc.scalar.copy)[part]
-            copy(
-                out=result[:, :, heads_per_bank * part : heads_per_bank * (part + 1)],
-                in_=by_h.rearrange("n h c -> n c h"),
-            )
+        plain = keep.tile([P, TILES * CHUNKS, CHUNK_HEADS, H], F32)
+        result = keep.tile([P, TILES * CHUNKS, CHUNK_HEADS, H], F32)
+        for group in range(CHUNKS):
+            heads = slice(CHUNK_HEADS * group, CHUNK_HEADS * (group + 1))
+            for j in range(2):
+                bank = psum.tile([P, BANK], F32, tag="bank")
+                for slot in range(CHUNK_HEADS):
+                    column = CHUNK_ROWS * group + CHUNK_HEADS * j + slot
+                    nc.tensor.transpose(bank[:, P * slot : P * (slot + 1)], weights[:, column, :], ident[:])
+                own = bank[:].rearrange("n (y g j x) -> n g j x y", y=CHUNK_HEADS, j=2, x=CHUNK_HEADS)[:, :, j, :, :]
+                if j == 0:
+                    nc.scalar.copy(out=plain[:, :, :, heads], in_=own)
+                else:
+                    nc.vector.tensor_tensor(out=result[:, :, :, heads], in0=own, in1=plain[:, :, :, heads], op=ALU.add)
         nc.sync.dma_start(
             out=out.rearrange("b n a h -> n b (a h)"),
-            in_=result[:].rearrange("n (t a) h -> n t (a h)", t=TILES),
+            in_=result[:].rearrange("n (t c) x h -> n t (c x h)", t=TILES),
         )

@@ -30,6 +30,7 @@ BANK = 512
 CHUNK_ROWS = 2 * CHUNK_HEADS
 BATCH = 16
 BANK_N = BANK // (2 * ROWS)
+RUN = 4
 
 SCALE = D ** -0.5
 LAM_INIT = 0.8 - 0.6 * math.exp(-0.3 * 12)
@@ -169,19 +170,20 @@ def tile_differentialattention_pa_kernel(
                     for j in range(2):
                         for h in range(CHUNK_HEADS):
                             nc.tensor.transpose(by_row[:, j, h, :], y[:, part, pair, j, h, :], ident_bf[:])
-                    by_n = bank[:].rearrange("k (r n) -> k n r", r=CHUNK_ROWS)
+                    src = bank[:].rearrange("k (r c i) -> k c r i", r=CHUNK_ROWS, i=RUN)
                     if c % 2 == 1:
                         copy = (nc.vector.tensor_copy, nc.scalar.copy)[pair]
                         first = ROWS * pair + row
-                        copy(out=k_parts[part][:, :, first : first + CHUNK_ROWS], in_=by_n)
+                        dst = k_parts[part][:, :, first : first + CHUNK_ROWS].rearrange("k (c i) r -> k c r i", i=RUN)
+                        copy(out=dst, in_=src)
                     else:
                         for s in range(2):
                             first = ROWS * (2 * pair + s) + row
-                            dst = q_parts[part][:, :, first : first + CHUNK_ROWS]
+                            dst = q_parts[part][:, :, first : first + CHUNK_ROWS].rearrange("k (c i) r -> k c r i", i=RUN)
                             if pair == 0:
-                                nc.vector.tensor_scalar_mul(out=dst, in0=by_n, scalar1=q_mask[:, s : s + 1])
+                                nc.vector.tensor_scalar_mul(out=dst, in0=src, scalar1=q_mask[:, s : s + 1])
                             else:
-                                nc.scalar.activation(out=dst, in_=by_n, func=ACT.Copy, scale=q_mask[:, s : s + 1])
+                                nc.scalar.activation(out=dst, in_=src, func=ACT.Copy, scale=q_mask[:, s : s + 1])
 
         n_chunks = 2 * CHUNKS
         y_tiles = [project(0)]
@@ -237,9 +239,9 @@ def tile_differentialattention_pa_kernel(
             nc.vector.reciprocal(out=inverse[:], in_=total[:])
             nc.vector.tensor_scalar_mul(out=inverse[:], in0=inverse[:], scalar1=coef[:, 0:1])
             nc.vector.tensor_tensor(
-                out=weights[:, :, BATCH * b : BATCH * (b + 1)],
-                in0=e[:].rearrange("q n m -> q m n"),
-                in1=inverse[:].unsqueeze(1).to_broadcast([P, ROWS, BATCH]),
+                out=weights[:, :, BATCH * b : BATCH * (b + 1)].rearrange("q (c i) n -> q c n i", i=RUN),
+                in0=e[:].rearrange("q n (c i) -> q c n i", i=RUN),
+                in1=inverse[:].unsqueeze(1).unsqueeze(3).to_broadcast([P, ROWS // RUN, BATCH, RUN]),
                 op=ALU.mult,
             )
 

@@ -47,7 +47,7 @@ def tile_differentialattention_pa_kernel(
         x_pool = ctx.enter_context(tc.tile_pool(name="x_pool", bufs=2))
         w_pool = ctx.enter_context(tc.tile_pool(name="w_pool", bufs=4))
         y_pool = ctx.enter_context(tc.tile_pool(name="y_pool", bufs=2))
-        soft = ctx.enter_context(tc.tile_pool(name="soft", bufs=3))
+        soft = ctx.enter_context(tc.tile_pool(name="soft", bufs=6))
         psum = ctx.enter_context(tc.psum_pool(name="psum", bufs=8))
         ctx.enter_context(tc.manual_schedule())
 
@@ -95,9 +95,17 @@ def tile_differentialattention_pa_kernel(
 
         x_codes = keep.tile([P, TILES, PASSES * P], U32, align_bytes=64)
         x_planes = keep.tile([P, TILES, PASSES * P], U8, align_bytes=64)
+        grouped_tiles = []
+
+        def quantise(t):
+            nc.vector.quantize_mx(
+                out=x_codes[:, t, :].bitcast(FP8X4), scales=x_planes[:, t, :], in_=grouped_tiles[t][:]
+            )
+
         for t in range(TILES):
             words = x_sb[t][:].bitcast(F32)
             grouped = x_pool.tile([P, PASSES * P * 4], BF16, tag="grouped", align_bytes=64)
+            grouped_tiles.append(grouped)
             grouped_words = grouped[:].bitcast(F32).rearrange("p (g n u) -> p g n u", g=PASSES, u=2)
             for half in range(2):
                 bank = psum.tile([P, BANK], F32, tag="bank")
@@ -113,9 +121,9 @@ def tile_differentialattention_pa_kernel(
                     out=grouped_words[:, 2 * half : 2 * half + 2, :, :],
                     in_=planes.rearrange("p g u n -> p g n u"),
                 )
-            nc.vector.quantize_mx(
-                out=x_codes[:, t, :].bitcast(FP8X4), scales=x_planes[:, t, :], in_=grouped[:]
-            )
+            if t > 0:
+                quantise(t - 1)
+        quantise(TILES - 1)
 
         ident_gjx = ident[:].rearrange("q (g j x) -> q g j x", j=2, x=CHUNK_HEADS)
         row_is = keep.tile([P, 2], F32)
@@ -225,37 +233,63 @@ def tile_differentialattention_pa_kernel(
                     nc.scalar.copy(out=e[rows, BANK_N * part : BANK_N * (part + 1), :], in_=sc[rows, :, pair, :])
             return e
 
-        def subtract_max(e):
-            top = soft.tile([P, BATCH], F32, tag="top")
-            nc.vector.tensor_reduce(out=top[:], in_=e[:], axis=AXIS.X, op=ALU.max)
-            nc.vector.tensor_tensor(
-                out=e[:], in0=e[:], in1=top[:].unsqueeze(2).to_broadcast([P, BATCH, ROWS]), op=ALU.subtract
+        tops, totals, inverses = {}, {}, {}
+
+        def find_max(b):
+            tops[b] = soft.tile([P, BATCH], F32, name="top", tag="top")
+            nc.vector.tensor_reduce(out=tops[b][:], in_=e_tiles[b][:], axis=AXIS.X, op=ALU.max)
+
+        def subtract_max(b):
+            e = e_tiles[b]
+            nc.gpsimd.tensor_tensor(
+                out=e[:], in0=e[:], in1=tops[b][:].unsqueeze(2).to_broadcast([P, BATCH, ROWS]), op=ALU.subtract
             )
 
-        def normalise(b, e):
-            total = soft.tile([P, BATCH], F32, tag="total")
-            nc.vector.tensor_reduce(out=total[:], in_=e[:], axis=AXIS.X, op=ALU.add)
-            inverse = soft.tile([P, BATCH], F32, tag="inverse")
-            nc.vector.reciprocal(out=inverse[:], in_=total[:])
-            nc.vector.tensor_scalar_mul(out=inverse[:], in0=inverse[:], scalar1=coef[:, 0:1])
+        def exponentials(b):
+            nc.scalar.activation(out=e_tiles[b][:], in_=e_tiles[b][:], func=ACT.Exp)
+
+        def add_up(b):
+            totals[b] = soft.tile([P, BATCH], F32, name="total", tag="total")
+            nc.vector.tensor_reduce(out=totals[b][:], in_=e_tiles[b][:], axis=AXIS.X, op=ALU.add)
+
+        def invert(b):
+            inverses[b] = soft.tile([P, BATCH], F32, name="inverse", tag="inverse")
+            nc.vector.reciprocal(out=inverses[b][:], in_=totals[b][:])
+
+        def apply_coef(b):
+            nc.vector.tensor_scalar_mul(out=inverses[b][:], in0=inverses[b][:], scalar1=coef[:, 0:1])
+
+        def normalise(b):
             nc.vector.tensor_tensor(
                 out=weights[:, :, BATCH * b : BATCH * (b + 1)].rearrange("q (c i) n -> q c n i", i=RUN),
-                in0=e[:].rearrange("q n (c i) -> q c n i", i=RUN),
-                in1=inverse[:].unsqueeze(1).unsqueeze(3).to_broadcast([P, ROWS // RUN, BATCH, RUN]),
+                in0=e_tiles[b][:].rearrange("q n (c i) -> q c n i", i=RUN),
+                in1=inverses[b][:].unsqueeze(1).unsqueeze(3).to_broadcast([P, ROWS // RUN, BATCH, RUN]),
                 op=ALU.mult,
             )
 
         batches = P // BATCH
         e_tiles = []
-        for b in range(batches + 2):
-            if b < batches:
-                e_tiles.append(scores(b))
-            if 1 <= b <= batches:
-                e = e_tiles[b - 1]
-                subtract_max(e)
-                nc.scalar.activation(out=e[:], in_=e[:], func=ACT.Exp)
-            if b >= 2:
-                normalise(b - 2, e_tiles[b - 2])
+
+        def in_range(b):
+            return 0 <= b < batches
+
+        for step in range(batches + 4):
+            if in_range(step):
+                e_tiles.append(scores(step))
+            if in_range(step - 3):
+                add_up(step - 3)
+            if in_range(step - 1):
+                find_max(step - 1)
+            if in_range(step - 3):
+                invert(step - 3)
+            if in_range(step - 1):
+                subtract_max(step - 1)
+            if in_range(step - 2):
+                exponentials(step - 2)
+            if in_range(step - 4):
+                normalise(step - 4)
+            if in_range(step - 3):
+                apply_coef(step - 3)
 
         plain = keep.tile([P, TILES * CHUNKS, CHUNK_HEADS, H], F32)
         result = keep.tile([P, TILES * CHUNKS, CHUNK_HEADS, H], F32)

@@ -17,20 +17,20 @@ AXIS = mybir.AxisListType
 
 P = 128
 TILES = 4
+PAIRS = TILES // 2
 C = 2048
 K_PASS = 512
 PASSES = C // K_PASS
 CHUNK = 512
-CHUNKS = 2048 // CHUNK
+CHUNKS = 2 * 2048 // CHUNK
 H = 16
 D = 64
 ROWS = 2 * H
 CHUNK_HEADS = CHUNK // (2 * D)
 BANK = 512
-CHUNK_ROWS = 2 * CHUNK_HEADS
-BATCH = 16
-BANK_N = BANK // (2 * ROWS)
-RUN = 4
+GROUPS = P // 2
+BATCH = BANK // (2 * ROWS)
+BATCHES = PAIRS * GROUPS // BATCH
 
 SCALE = D ** -0.5
 LAM_INIT = 0.8 - 0.6 * math.exp(-0.3 * 12)
@@ -45,67 +45,90 @@ def tile_differentialattention_pa_kernel(
     with ExitStack() as ctx:
         keep = ctx.enter_context(tc.tile_pool(name="keep", bufs=1))
         x_pool = ctx.enter_context(tc.tile_pool(name="x_pool", bufs=2))
-        w_pool = ctx.enter_context(tc.tile_pool(name="w_pool", bufs=4))
-        y_pool = ctx.enter_context(tc.tile_pool(name="y_pool", bufs=2))
+        y_pool = ctx.enter_context(tc.tile_pool(name="y_pool", bufs=3))
         soft = ctx.enter_context(tc.tile_pool(name="soft", bufs=6))
         psum = ctx.enter_context(tc.psum_pool(name="psum", bufs=8))
         ctx.enter_context(tc.manual_schedule())
 
-        x_sb = []
-        for t in range(TILES):
-            x_tile = keep.tile([P, C], BF16, name="x_sb%d" % t)
+        x_sb = {}
+
+        def load_x(t):
+            x_tile = x_pool.tile([P, C], BF16, tag="x_sb")
             nc.sync.dma_start(out=x_tile[:], in_=x[t])
-            x_sb.append(x_tile)
+            x_sb[t] = x_tile
 
-        lam_vecs = keep.tile([P, 4, D], BF16)
-        for v, vec in enumerate((lq1, lq2, lk1, lk2)):
-            nc.scalar.dma_start(out=lam_vecs[:, v, :], in_=vec.partition_broadcast(P))
-
-        def load_planes(name, scales):
+        w_planes = []
+        for name in ("q", "k"):
             planes = keep.tile([P, 2048], U8, name="w_planes_" + name, align_bytes=64)
             nc.vector.memset(planes[:].bitcast(I32), 0)
+            w_planes.append(planes)
+
+        def load_planes(which, scales):
             for quad in range(4):
                 nc.sync.dma_start(
-                    out=planes[32 * quad : 32 * quad + 16, :].bitcast(I32),
+                    out=w_planes[which][32 * quad : 32 * quad + 16, :].bitcast(I32),
                     in_=scales[:, 4 * quad : 4 * quad + 4, :].bitcast(I32),
                 )
-            return planes
 
-        def load_chunk(c):
+        chunk_words = {}
+
+        def load_chunk(c, pieces):
             words = (Wq_words, Wk_words)[c % 2]
             first = 4 * CHUNK * (c // 2)
-            w = w_pool.tile([P, PASSES, 4 * CHUNK], U8, tag="w", align_bytes=64)
-            nc.sync.dma_start(
-                out=w[:].bitcast(I32),
-                in_=words.rearrange("g p n t -> p g (n t)")[:, :, first : first + 4 * CHUNK].bitcast(I32),
-            )
-            return w
+            w = keep.tile([P, PASSES, 4 * CHUNK], U8, name="w%d" % c, align_bytes=64)
+            src = words.rearrange("g p n t -> p g (n t)")[:, :, first : first + 4 * CHUNK]
+            step = PASSES // pieces
+            for g in range(0, PASSES, step):
+                nc.sync.dma_start(out=w[:, g : g + step, :].bitcast(I32), in_=src[:, g : g + step, :].bitcast(I32))
+            chunk_words[c] = w
 
-        q_planes = load_planes("q", Wq_scales)
-        chunk_words = [load_chunk(0)]
-        k_planes = load_planes("k", Wk_scales)
-        w_planes = (q_planes, k_planes)
-        for c in range(1, 4):
-            chunk_words.append(load_chunk(c))
+        load_x(0)
+        load_x(1)
+        load_planes(0, Wq_scales)
+        load_chunk(0, PASSES)
+        load_planes(1, Wk_scales)
+        for c in range(1, 5):
+            load_chunk(c, 1)
+        load_x(2)
+        load_x(3)
+        for c in range(5, CHUNKS):
+            load_chunk(c, 1)
+        lam_vecs = keep.tile([P, 4, D], BF16)
+        for v, vec in enumerate((lq1, lq2, lk1, lk2)):
+            nc.sync.dma_start(out=lam_vecs[:, v, :], in_=vec.partition_broadcast(P))
 
         ident = keep.tile([P, P], F32)
         masks.make_identity(nc, ident[:])
-        ident_bf = keep.tile([P, P], BF16)
-        masks.make_identity(nc, ident_bf[:])
+        warm = keep.tile([P, 2], F32)
+        nc.vector.memset(warm[:, 0:1], 0.0)
+        nc.scalar.activation(out=warm[:, 1:2], in_=warm[:, 0:1], func=ACT.Exp)
+
+        q_tiles = [[keep.tile([P, GROUPS, P], BF16, name="q%d%d" % (pair, part)) for part in range(2)] for pair in range(PAIRS)]
+        k_tiles = [[keep.tile([P, GROUPS, 2 * ROWS], BF16, name="k%d%d" % (pair, part)) for part in range(2)] for pair in range(PAIRS)]
+
+        def flat_words(tile_):
+            return tile_[:].rearrange("k m c -> k (m c)").bitcast(F32)
+
+        def zero_q(pair, part, piece, pieces):
+            words = flat_words(q_tiles[pair][part])
+            width = GROUPS * P // 2 // pieces
+            nc.vector.memset(words[:, width * piece : width * (piece + 1)], 0.0)
+
+        zero_q(0, 0, 0, 1)
 
         x_codes = keep.tile([P, TILES, PASSES * P], U32, align_bytes=64)
         x_planes = keep.tile([P, TILES, PASSES * P], U8, align_bytes=64)
-        grouped_tiles = []
+        grouped_tiles = {}
 
         def quantise(t):
             nc.vector.quantize_mx(
                 out=x_codes[:, t, :].bitcast(FP8X4), scales=x_planes[:, t, :], in_=grouped_tiles[t][:]
             )
 
-        for t in range(TILES):
+        def transpose_x(t):
             words = x_sb[t][:].bitcast(F32)
             grouped = x_pool.tile([P, PASSES * P * 4], BF16, tag="grouped", align_bytes=64)
-            grouped_tiles.append(grouped)
+            grouped_tiles[t] = grouped
             grouped_words = grouped[:].bitcast(F32).rearrange("p (g n u) -> p g n u", g=PASSES, u=2)
             for half in range(2):
                 bank = psum.tile([P, BANK], F32, tag="bank")
@@ -121,191 +144,213 @@ def tile_differentialattention_pa_kernel(
                     out=grouped_words[:, 2 * half : 2 * half + 2, :, :],
                     in_=planes.rearrange("p g u n -> p g n u"),
                 )
-            if t > 0:
-                quantise(t - 1)
-        quantise(TILES - 1)
 
-        ident_gjx = ident[:].rearrange("q (g j x) -> q g j x", j=2, x=CHUNK_HEADS)
-        row_is = keep.tile([P, 2], F32)
-        for j in range(2):
-            nc.vector.tensor_reduce(out=row_is[:, j : j + 1], in_=ident_gjx[:, :, j, :], axis=AXIS.XY, op=ALU.add)
-        q_mask = keep.tile([P, 2], F32)
-        nc.vector.tensor_reduce(
-            out=q_mask[:], in_=ident[:].rearrange("q (s d) -> q s d", s=2), axis=AXIS.X, op=ALU.add
-        )
-        nc.vector.tensor_scalar_mul(out=q_mask[:], in0=q_mask[:], scalar1=SCALE)
-        lam_prod = keep.tile([P, 2, D], F32)
-        nc.vector.tensor_tensor(out=lam_prod[:], in0=lam_vecs[:, 0:2, :], in1=lam_vecs[:, 2:4, :], op=ALU.mult)
-        lam_dots = keep.tile([P, 2], F32)
-        nc.vector.tensor_reduce(out=lam_dots[:], in_=lam_prod[:], axis=AXIS.X, op=ALU.add)
-        lam_exps = keep.tile([P, 2], F32)
-        nc.scalar.activation(out=lam_exps[:], in_=lam_dots[:], func=ACT.Exp)
+        transpose_x(0)
+        quantise(0)
+        transpose_x(1)
+        quantise(1)
+        zero_q(0, 1, 0, 1)
 
-        q_parts = [keep.tile([P, P, TILES * ROWS], BF16, name="q_" + part) for part in ("hi", "lo")]
-        k_parts = [keep.tile([P, P, 2 * ROWS], BF16, name="k_" + part) for part in ("hi", "lo")]
+        STEPS = PAIRS * CHUNKS
+        acc_tiles = {}
+        y_tiles = {}
+        t_banks = {}
 
-        def project(c):
+        def project(i, s):
+            pair, c = divmod(i, CHUNKS)
+            t = 2 * pair + s
             w = chunk_words[c]
             planes = w_planes[c % 2]
             cols = slice(CHUNK * (c // 2), CHUNK * (c // 2 + 1))
-            y = y_pool.tile([P, 2, 2, 2, CHUNK_HEADS, 2 * D], BF16, tag="y")
-            for t in range(TILES):
-                acc = psum.tile([P, BANK], F32, tag="bank")
-                for g in range(PASSES):
-                    nc.tensor.matmul_mx(
-                        out=acc[:],
-                        lhsT=x_codes[:, t, P * g : P * (g + 1)].bitcast(FP8X4),
-                        lhsT_scale=x_planes[:, t, P * g : P * (g + 1)],
-                        rhs=w[:, g, :].bitcast(FP8X4),
-                        rhs_scale=planes[4 * g : P, cols],
-                        start=(g == 0),
-                        stop=(g == PASSES - 1),
-                    )
-                by_row = acc[:].rearrange("p (h d j) -> p j h d", d=D, j=2)
-                side = slice(D * (t % 2), D * (t % 2 + 1))
-                hi = y[:, 0, t // 2, :, :, side]
-                lo = y[:, 1, t // 2, :, :, side]
-                nc.scalar.copy(out=hi, in_=by_row)
-                nc.vector.tensor_tensor(out=lo, in0=by_row, in1=hi, op=ALU.subtract)
-            return y
+            acc = psum.tile([P, BANK], F32, tag="bank")
+            for g in range(PASSES):
+                nc.tensor.matmul_mx(
+                    out=acc[:],
+                    lhsT=x_codes[:, t, P * g : P * (g + 1)].bitcast(FP8X4),
+                    lhsT_scale=x_planes[:, t, P * g : P * (g + 1)],
+                    rhs=w[:, g, :].bitcast(FP8X4),
+                    rhs_scale=planes[4 * g : P, cols],
+                    start=(g == 0),
+                    stop=(g == PASSES - 1),
+                )
+            acc_tiles[(i, s)] = acc
 
-        def transpose_chunk(c, y):
-            row = CHUNK_ROWS * (c // 2)
-            for part in range(2):
-                for pair in range(2):
-                    bank = psum.tile([P, 2 * BANK], BF16, tag="bank")
-                    by_row = bank[:].rearrange("k (j h n) -> k j h n", j=2, h=CHUNK_HEADS)
-                    for j in range(2):
-                        for h in range(CHUNK_HEADS):
-                            nc.tensor.transpose(by_row[:, j, h, :], y[:, part, pair, j, h, :], ident_bf[:])
-                    src = bank[:].rearrange("k (r c i) -> k c r i", r=CHUNK_ROWS, i=RUN)
-                    if c % 2 == 1:
-                        copy = (nc.vector.tensor_copy, nc.scalar.copy)[pair]
-                        first = ROWS * pair + row
-                        dst = k_parts[part][:, :, first : first + CHUNK_ROWS].rearrange("k (c i) r -> k c r i", i=RUN)
-                        copy(out=dst, in_=src)
-                    else:
-                        for s in range(2):
-                            first = ROWS * (2 * pair + s) + row
-                            dst = q_parts[part][:, :, first : first + CHUNK_ROWS].rearrange("k (c i) r -> k c r i", i=RUN)
-                            if pair == 0:
-                                nc.vector.tensor_scalar_mul(out=dst, in0=src, scalar1=q_mask[:, s : s + 1])
-                            else:
-                                nc.scalar.activation(out=dst, in_=src, func=ACT.Copy, scale=q_mask[:, s : s + 1])
+        def new_y(i):
+            y = y_pool.tile([P, 2, CHUNK_HEADS, 2, 2 * D], BF16, tag="y")
+            y_tiles[i] = y
 
-        n_chunks = 2 * CHUNKS
-        y_tiles = [project(0)]
-        for c in range(1, n_chunks):
-            if c + 3 < n_chunks:
-                chunk_words.append(load_chunk(c + 3))
-            y_tiles.append(project(c))
-            transpose_chunk(c - 1, y_tiles[c - 1])
-        transpose_chunk(n_chunks - 1, y_tiles[n_chunks - 1])
+        def split_hi(i, s):
+            by_head = acc_tiles[(i, s)][:].rearrange("p (h e) -> p h e", h=CHUNK_HEADS)
+            nc.scalar.copy(out=y_tiles[i][:, 0, :, s, :], in_=by_head)
 
-        neg_lam = keep.tile([P, 1], F32)
-        nc.vector.tensor_tensor(out=neg_lam[:], in0=lam_exps[:, 1:2], in1=lam_exps[:, 0:1], op=ALU.subtract)
-        nc.vector.tensor_scalar_add(out=neg_lam[:], in0=neg_lam[:], scalar1=-LAM_INIT)
-        coef = keep.tile([P, 1], F32)
-        nc.vector.scalar_tensor_tensor(
-            out=coef[:], in0=row_is[:, 1:2], scalar=neg_lam[:, 0:1], in1=row_is[:, 0:1], op0=ALU.mult, op1=ALU.add
-        )
-
-        weights = keep.tile([P, ROWS, P], F32)
-
-        def scores(b):
-            e = soft.tile([P, BATCH, ROWS], F32, tag="e")
-            for part in range(BATCH // BANK_N):
-                bank = psum.tile([P, BANK], F32, tag="bank")
-                sc = bank[:].rearrange("q (n a m) -> q n a m", a=2, m=ROWS)
-                for i in range(BANK_N):
-                    n = BATCH * b + BANK_N * part + i
-                    terms = ((0, 0), (0, 1), (1, 0))
-                    for term, (q_part, k_part) in enumerate(terms):
-                        nc.tensor.matmul(
-                            out=bank[:, 2 * ROWS * i : 2 * ROWS * (i + 1)],
-                            lhsT=q_parts[q_part][:, n, :],
-                            rhs=k_parts[k_part][:, n, :],
-                            start=(term == 0),
-                            stop=(term == len(terms) - 1),
-                        )
-                for pair in range(2):
-                    rows = slice(64 * pair, 64 * (pair + 1))
-                    nc.scalar.copy(out=e[rows, BANK_N * part : BANK_N * (part + 1), :], in_=sc[rows, :, pair, :])
-            return e
-
-        tops, totals, inverses = {}, {}, {}
-
-        def find_max(b):
-            tops[b] = soft.tile([P, BATCH], F32, name="top", tag="top")
-            nc.vector.tensor_reduce(out=tops[b][:], in_=e_tiles[b][:], axis=AXIS.X, op=ALU.max)
-
-        def subtract_max(b):
-            e = e_tiles[b]
-            nc.gpsimd.tensor_tensor(
-                out=e[:], in0=e[:], in1=tops[b][:].unsqueeze(2).to_broadcast([P, BATCH, ROWS]), op=ALU.subtract
+        def split_lo(i, s):
+            by_head = acc_tiles[(i, s)][:].rearrange("p (h e) -> p h e", h=CHUNK_HEADS)
+            nc.vector.tensor_tensor(
+                out=y_tiles[i][:, 1, :, s, :], in0=by_head, in1=y_tiles[i][:, 0, :, s, :], op=ALU.subtract
             )
 
-        def exponentials(b):
-            nc.scalar.activation(out=e_tiles[b][:], in_=e_tiles[b][:], func=ACT.Exp)
+        def transpose_y(i):
+            y = y_tiles[i]
+            banks = []
+            for part in range(2):
+                bank = psum.tile([P, BANK], F32, tag="bank")
+                for h in range(CHUNK_HEADS):
+                    words = y[:, part, h, :, :].rearrange("p s e -> p (s e)").bitcast(F32)
+                    nc.tensor.transpose(bank[:, P * h : P * (h + 1)], words, ident[:])
+                banks.append(bank)
+            t_banks[i] = banks
 
-        def add_up(b):
-            totals[b] = soft.tile([P, BATCH], F32, name="total", tag="total")
-            nc.vector.tensor_reduce(out=totals[b][:], in_=e_tiles[b][:], axis=AXIS.X, op=ALU.add)
+        def sort_rows(i):
+            pair, c = divmod(i, CHUNKS)
+            h0 = CHUNK_HEADS * (c // 2)
+            for part in range(2):
+                copy = (nc.vector.tensor_copy, nc.scalar.copy)[part]
+                src = t_banks[i][part][:].rearrange("k (h n) -> k n h", h=CHUNK_HEADS)
+                if c % 2 == 1:
+                    dst = flat_words(k_tiles[pair][part]).rearrange("k (n x) -> k n x", x=H)
+                    copy(out=dst[:, :, h0 : h0 + CHUNK_HEADS], in_=src)
+                else:
+                    dst = flat_words(q_tiles[pair][part]).rearrange("k (n x) -> k n x", x=2 * H)
+                    for s in range(2):
+                        rows = slice(D * s, D * (s + 1))
+                        first = H * s + h0
+                        copy(out=dst[rows, :, first : first + CHUNK_HEADS], in_=src[rows, :, :])
 
-        def invert(b):
-            inverses[b] = soft.tile([P, BATCH], F32, name="inverse", tag="inverse")
-            nc.vector.reciprocal(out=inverses[b][:], in_=totals[b][:])
+        w_all = keep.tile([P, ROWS, P], F32)
+        e_tiles, tops, totals, inverses = {}, {}, {}, {}
 
-        def apply_coef(b):
-            nc.vector.tensor_scalar_mul(out=inverses[b][:], in0=inverses[b][:], scalar1=coef[:, 0:1])
+        def in_range(k):
+            return 0 <= k < BATCHES
 
-        def normalise(b):
+        def scores(k):
+            pair, b = divmod(k, GROUPS // BATCH)
+            bank = psum.tile([P, BANK], F32, tag="bank")
+            for g in range(BATCH):
+                m = BATCH * b + g
+                terms = ((0, 0), (0, 1), (1, 0))
+                for term, (q_part, k_part) in enumerate(terms):
+                    nc.tensor.matmul(
+                        out=bank[:, 2 * ROWS * g : 2 * ROWS * (g + 1)],
+                        lhsT=q_tiles[pair][q_part][:, m, :],
+                        rhs=k_tiles[pair][k_part][:, m, :],
+                        start=(term == 0),
+                        stop=(term == len(terms) - 1),
+                    )
+            e = soft.tile([P, BATCH, ROWS], F32, tag="e")
+            sc = bank[:].rearrange("q (g u r) -> q g u r", u=2, r=ROWS)
+            for u in range(2):
+                rows = slice(64 * u, 64 * (u + 1))
+                nc.scalar.copy(out=e[rows, :, :], in_=sc[rows, :, u, :])
+            e_tiles[k] = e
+
+        def find_max(k):
+            top = soft.tile([P, BATCH], F32, tag="top")
+            nc.vector.tensor_reduce(out=top[:], in_=e_tiles[k][:], axis=AXIS.X, op=ALU.max)
+            tops[k] = top
+
+        def subtract_max(k):
+            e = e_tiles[k]
+            nc.gpsimd.tensor_tensor(
+                out=e[:], in0=e[:], in1=tops[k][:].unsqueeze(2).to_broadcast([P, BATCH, ROWS]), op=ALU.subtract
+            )
+
+        def exponentials(k):
+            nc.scalar.activation(out=e_tiles[k][:], in_=e_tiles[k][:], func=ACT.Exp, scale=SCALE)
+
+        def add_up(k):
+            total = soft.tile([P, BATCH], F32, tag="total")
+            nc.vector.tensor_reduce(out=total[:], in_=e_tiles[k][:], axis=AXIS.X, op=ALU.add)
+            totals[k] = total
+
+        def invert(k):
+            inverse = soft.tile([P, BATCH], F32, tag="inverse")
+            nc.vector.reciprocal(out=inverse[:], in_=totals[k][:])
+            inverses[k] = inverse
+
+        def normalise(k):
             nc.vector.tensor_tensor(
-                out=weights[:, :, BATCH * b : BATCH * (b + 1)].rearrange("q (c i) n -> q c n i", i=RUN),
-                in0=e_tiles[b][:].rearrange("q n (c i) -> q c n i", i=RUN),
-                in1=inverses[b][:].unsqueeze(1).unsqueeze(3).to_broadcast([P, ROWS // RUN, BATCH, RUN]),
+                out=w_all[:, :, BATCH * k : BATCH * (k + 1)],
+                in0=e_tiles[k][:].rearrange("q g r -> q r g"),
+                in1=inverses[k][:].unsqueeze(1).to_broadcast([P, ROWS, BATCH]),
                 op=ALU.mult,
             )
 
-        batches = P // BATCH
-        e_tiles = []
+        neg_lam = keep.tile([P, 1], F32)
 
-        def in_range(b):
-            return 0 <= b < batches
+        def lam_value():
+            lam_prod = keep.tile([P, 2, D], F32)
+            nc.vector.tensor_tensor(out=lam_prod[:], in0=lam_vecs[:, 0:2, :], in1=lam_vecs[:, 2:4, :], op=ALU.mult)
+            lam_dots = keep.tile([P, 2], F32)
+            nc.vector.tensor_reduce(out=lam_dots[:], in_=lam_prod[:], axis=AXIS.X, op=ALU.add)
+            lam_exps = keep.tile([P, 2], F32)
+            nc.scalar.activation(out=lam_exps[:], in_=lam_dots[:], func=ACT.Exp)
+            nc.vector.tensor_tensor(out=neg_lam[:], in0=lam_exps[:, 1:2], in1=lam_exps[:, 0:1], op=ALU.subtract)
+            nc.vector.tensor_scalar_add(out=neg_lam[:], in0=neg_lam[:], scalar1=-LAM_INIT)
 
-        for step in range(batches + 4):
-            if in_range(step):
-                e_tiles.append(scores(step))
-            if in_range(step - 3):
-                add_up(step - 3)
-            if in_range(step - 1):
-                find_max(step - 1)
-            if in_range(step - 3):
-                invert(step - 3)
-            if in_range(step - 1):
-                subtract_max(step - 1)
-            if in_range(step - 2):
-                exponentials(step - 2)
-            if in_range(step - 4):
-                normalise(step - 4)
-            if in_range(step - 3):
-                apply_coef(step - 3)
+        FIRST_TICK = CHUNKS + 1
+        LAG = 4
+        for i in range(FIRST_TICK + BATCHES + LAG):
+            k = i - FIRST_TICK
+            if i < STEPS:
+                new_y(i)
+                project(i, 0)
+                project(i, 1)
+            if 0 <= i - 2 < STEPS:
+                sort_rows(i - 2)
+            if in_range(k - 3):
+                add_up(k - 3)
+            if in_range(k - 1):
+                find_max(k - 1)
+            if i < STEPS:
+                split_hi(i, 0)
+                split_lo(i, 0)
+            if in_range(k - 1):
+                subtract_max(k - 1)
+            if in_range(k - 2):
+                exponentials(k - 2)
+            if in_range(k - 3):
+                invert(k - 3)
+            if in_range(k - 4):
+                normalise(k - 4)
+            if i in (6, 7):
+                quantise(i - 4)
+            if i < STEPS:
+                split_hi(i, 1)
+                split_lo(i, 1)
+            if 1 <= i <= 4:
+                zero_q(1, (i - 1) // 2, (i - 1) % 2, 2)
+            if in_range(k):
+                scores(k)
+            if 0 <= i - 1 < STEPS:
+                transpose_y(i - 1)
+            if i in (5, 6):
+                transpose_x(i - 3)
+            if i == 10:
+                lam_value()
 
-        plain = keep.tile([P, TILES * CHUNKS, CHUNK_HEADS, H], F32)
-        result = keep.tile([P, TILES * CHUNKS, CHUNK_HEADS, H], F32)
-        for group in range(CHUNKS):
-            heads = slice(CHUNK_HEADS * group, CHUNK_HEADS * (group + 1))
+        plain = keep.tile([P, 4 * H, H], F32)
+        result = keep.tile([P, 4 * H, H], F32)
+        for quad in range(H // 4):
+            heads = slice(4 * quad, 4 * (quad + 1))
             for j in range(2):
                 bank = psum.tile([P, BANK], F32, tag="bank")
-                for slot in range(CHUNK_HEADS):
-                    column = CHUNK_ROWS * group + CHUNK_HEADS * j + slot
-                    nc.tensor.transpose(bank[:, P * slot : P * (slot + 1)], weights[:, column, :], ident[:])
-                own = bank[:].rearrange("n (y g j x) -> n g j x y", y=CHUNK_HEADS, j=2, x=CHUNK_HEADS)[:, :, j, :, :]
+                for slot in range(4):
+                    column = 2 * (4 * quad + slot) + j
+                    nc.tensor.transpose(bank[:, P * slot : P * (slot + 1)], w_all[:, column, :], ident[:])
+                own = bank[:].rearrange("n (y a j) -> n a j y", y=4, j=2)[:, :, j, :]
                 if j == 0:
-                    nc.scalar.copy(out=plain[:, :, :, heads], in_=own)
+                    nc.scalar.copy(out=plain[:, :, heads], in_=own)
                 else:
-                    nc.vector.tensor_tensor(out=result[:, :, :, heads], in0=own, in1=plain[:, :, :, heads], op=ALU.add)
-        nc.sync.dma_start(
-            out=out.rearrange("b n a h -> n b (a h)"),
-            in_=result[:].rearrange("n (t c) x h -> n t (c x h)", t=TILES),
-        )
+                    nc.vector.scalar_tensor_tensor(
+                        out=result[:, :, heads], in0=own, scalar=neg_lam[:, 0:1], in1=plain[:, :, heads],
+                        op0=ALU.mult, op1=ALU.add,
+                    )
+        out_view = out.rearrange("(w s) (m u) a h -> w u m s (a h)", s=2, u=2)
+        for pair in range(PAIRS):
+            for u in range(2):
+                nc.sync.dma_start(
+                    out=out_view[pair, u],
+                    in_=result[GROUPS * pair : GROUPS * (pair + 1), 2 * H * u : 2 * H * (u + 1), :].rearrange(
+                        "m (s a) h -> m s (a h)", s=2
+                    ),
+                )

@@ -30,7 +30,9 @@ CHUNK_HEADS = CHUNK // (2 * D)
 BANK = 512
 GROUPS = P // 2
 BATCH = BANK // (2 * ROWS)
-BATCHES = PAIRS * GROUPS // BATCH
+PAIR_BATCHES = GROUPS // BATCH
+FIRST_TICK_STEP = 11
+RUN = 4
 
 SCALE = D ** -0.5
 LAM_INIT = 0.8 - 0.6 * math.exp(-0.3 * 12)
@@ -72,9 +74,12 @@ def tile_differentialattention_pa_kernel(
 
         chunk_words = {}
 
+        def is_k(c):
+            return 1 if c < 4 else 0
+
         def load_chunk(c, pieces):
-            words = (Wq_words, Wk_words)[c % 2]
-            first = 4 * CHUNK * (c // 2)
+            words = (Wq_words, Wk_words)[is_k(c)]
+            first = 4 * CHUNK * (c % 4)
             w = keep.tile([P, PASSES, 4 * CHUNK], U8, name="w%d" % c, align_bytes=64)
             src = words.rearrange("g p n t -> p g (n t)")[:, :, first : first + 4 * CHUNK]
             step = PASSES // pieces
@@ -84,14 +89,15 @@ def tile_differentialattention_pa_kernel(
 
         load_x(0)
         load_x(1)
-        load_planes(0, Wq_scales)
-        load_chunk(0, PASSES)
         load_planes(1, Wk_scales)
-        for c in range(1, 5):
+        load_chunk(0, PASSES)
+        load_chunk(1, PASSES)
+        load_planes(0, Wq_scales)
+        for c in range(2, 6):
             load_chunk(c, 1)
         load_x(2)
         load_x(3)
-        for c in range(5, CHUNKS):
+        for c in range(6, CHUNKS):
             load_chunk(c, 1)
         lam_vecs = keep.tile([P, 4, D], BF16)
         for v, vec in enumerate((lq1, lq2, lk1, lk2)):
@@ -109,21 +115,24 @@ def tile_differentialattention_pa_kernel(
         def flat_words(tile_):
             return tile_[:].rearrange("k m c -> k (m c)").bitcast(F32)
 
-        def zero_q(pair, part, piece, pieces):
-            words = flat_words(q_tiles[pair][part])
-            width = GROUPS * P // 2 // pieces
-            nc.vector.memset(words[:, width * piece : width * (piece + 1)], 0.0)
-
-        zero_q(0, 0, 0, 1)
+        for pair in range(PAIRS):
+            for part in range(2):
+                words = flat_words(q_tiles[pair][part])
+                for piece in range(GROUPS * P // 2 // BANK):
+                    nc.gpsimd.memset(words[:, BANK * piece : BANK * (piece + 1)], 0.0)
 
         x_codes = keep.tile([P, TILES, PASSES * P], U32, align_bytes=64)
         x_planes = keep.tile([P, TILES, PASSES * P], U8, align_bytes=64)
         grouped_tiles = {}
 
         def quantise(t):
-            nc.vector.quantize_mx(
-                out=x_codes[:, t, :].bitcast(FP8X4), scales=x_planes[:, t, :], in_=grouped_tiles[t][:]
-            )
+            for half in range(2):
+                cols = slice(2 * P * half, 2 * P * (half + 1))
+                nc.vector.quantize_mx(
+                    out=x_codes[:, t, cols].bitcast(FP8X4),
+                    scales=x_planes[:, t, cols],
+                    in_=grouped_tiles[t][:, 8 * P * half : 8 * P * (half + 1)],
+                )
 
         def transpose_x(t):
             words = x_sb[t][:].bitcast(F32)
@@ -149,19 +158,22 @@ def tile_differentialattention_pa_kernel(
         quantise(0)
         transpose_x(1)
         quantise(1)
-        zero_q(0, 1, 0, 1)
 
         STEPS = PAIRS * CHUNKS
         acc_tiles = {}
         y_tiles = {}
         t_banks = {}
 
+        def pair_chunk(i):
+            pair, place = divmod(i, CHUNKS)
+            return pair, (place + 4 * pair) % CHUNKS
+
         def project(i, s):
-            pair, c = divmod(i, CHUNKS)
+            pair, c = pair_chunk(i)
             t = 2 * pair + s
             w = chunk_words[c]
-            planes = w_planes[c % 2]
-            cols = slice(CHUNK * (c // 2), CHUNK * (c // 2 + 1))
+            planes = w_planes[is_k(c)]
+            cols = slice(CHUNK * (c % 4), CHUNK * (c % 4 + 1))
             acc = psum.tile([P, BANK], F32, tag="bank")
             for g in range(PASSES):
                 nc.tensor.matmul_mx(
@@ -201,29 +213,26 @@ def tile_differentialattention_pa_kernel(
             t_banks[i] = banks
 
         def sort_rows(i):
-            pair, c = divmod(i, CHUNKS)
-            h0 = CHUNK_HEADS * (c // 2)
+            pair, c = pair_chunk(i)
+            h0 = CHUNK_HEADS * (c % 4)
             for part in range(2):
                 copy = (nc.vector.tensor_copy, nc.scalar.copy)[part]
-                src = t_banks[i][part][:].rearrange("k (h n) -> k n h", h=CHUNK_HEADS)
-                if c % 2 == 1:
-                    dst = flat_words(k_tiles[pair][part]).rearrange("k (n x) -> k n x", x=H)
-                    copy(out=dst[:, :, h0 : h0 + CHUNK_HEADS], in_=src)
+                src = t_banks[i][part][:].rearrange("k (h c i) -> k c h i", h=CHUNK_HEADS, i=RUN)
+                if is_k(c):
+                    dst = flat_words(k_tiles[pair][part]).rearrange("k (c i x) -> k c x i", i=RUN, x=H)
+                    copy(out=dst[:, :, h0 : h0 + CHUNK_HEADS, :], in_=src)
                 else:
-                    dst = flat_words(q_tiles[pair][part]).rearrange("k (n x) -> k n x", x=2 * H)
+                    dst = flat_words(q_tiles[pair][part]).rearrange("k (c i x) -> k c x i", i=RUN, x=2 * H)
                     for s in range(2):
                         rows = slice(D * s, D * (s + 1))
                         first = H * s + h0
-                        copy(out=dst[rows, :, first : first + CHUNK_HEADS], in_=src[rows, :, :])
+                        copy(out=dst[rows, :, first : first + CHUNK_HEADS, :], in_=src[rows, :, :, :])
 
         w_all = keep.tile([P, ROWS, P], F32)
         e_tiles, tops, totals, inverses = {}, {}, {}, {}
 
-        def in_range(k):
-            return 0 <= k < BATCHES
-
         def scores(k):
-            pair, b = divmod(k, GROUPS // BATCH)
+            pair, b = divmod(k, PAIR_BATCHES)
             bank = psum.tile([P, BANK], F32, tag="bank")
             for g in range(BATCH):
                 m = BATCH * b + g
@@ -269,9 +278,9 @@ def tile_differentialattention_pa_kernel(
 
         def normalise(k):
             nc.vector.tensor_tensor(
-                out=w_all[:, :, BATCH * k : BATCH * (k + 1)],
-                in0=e_tiles[k][:].rearrange("q g r -> q r g"),
-                in1=inverses[k][:].unsqueeze(1).to_broadcast([P, ROWS, BATCH]),
+                out=w_all[:, :, BATCH * k : BATCH * (k + 1)].rearrange("q (c i) g -> q c g i", i=RUN),
+                in0=e_tiles[k][:].rearrange("q g (c i) -> q c g i", i=RUN),
+                in1=inverses[k][:].unsqueeze(1).unsqueeze(3).to_broadcast([P, ROWS // RUN, BATCH, RUN]),
                 op=ALU.mult,
             )
 
@@ -287,8 +296,31 @@ def tile_differentialattention_pa_kernel(
             nc.vector.tensor_tensor(out=neg_lam[:], in0=lam_exps[:, 1:2], in1=lam_exps[:, 0:1], op=ALU.subtract)
             nc.vector.tensor_scalar_add(out=neg_lam[:], in0=neg_lam[:], scalar1=-LAM_INIT)
 
-        FIRST_TICK = CHUNKS + 1
         LAG = 4
+        BATCHES = PAIRS * PAIR_BATCHES
+
+        def front(k):
+            def live(b):
+                return 0 <= b < BATCHES
+
+            if live(k - 3):
+                add_up(k - 3)
+            if live(k - 1):
+                find_max(k - 1)
+            if live(k - 3):
+                invert(k - 3)
+            if live(k - 4):
+                normalise(k - 4)
+            if live(k - 1):
+                subtract_max(k - 1)
+            if live(k - 2):
+                exponentials(k - 2)
+
+        def back(k):
+            if 0 <= k < BATCHES:
+                scores(k)
+
+        FIRST_TICK = FIRST_TICK_STEP
         for i in range(FIRST_TICK + BATCHES + LAG):
             k = i - FIRST_TICK
             if i < STEPS:
@@ -297,35 +329,21 @@ def tile_differentialattention_pa_kernel(
                 project(i, 1)
             if 0 <= i - 2 < STEPS:
                 sort_rows(i - 2)
-            if in_range(k - 3):
-                add_up(k - 3)
-            if in_range(k - 1):
-                find_max(k - 1)
+            front(k)
             if i < STEPS:
                 split_hi(i, 0)
                 split_lo(i, 0)
-            if in_range(k - 1):
-                subtract_max(k - 1)
-            if in_range(k - 2):
-                exponentials(k - 2)
-            if in_range(k - 3):
-                invert(k - 3)
-            if in_range(k - 4):
-                normalise(k - 4)
             if i in (6, 7):
                 quantise(i - 4)
             if i < STEPS:
                 split_hi(i, 1)
                 split_lo(i, 1)
-            if 1 <= i <= 4:
-                zero_q(1, (i - 1) // 2, (i - 1) % 2, 2)
-            if in_range(k):
-                scores(k)
+            back(k)
             if 0 <= i - 1 < STEPS:
                 transpose_y(i - 1)
             if i in (5, 6):
                 transpose_x(i - 3)
-            if i == 10:
+            if i == 9:
                 lam_value()
 
         plain = keep.tile([P, 4 * H, H], F32)

@@ -115,11 +115,25 @@ def tile_differentialattention_pa_kernel(
         def flat_words(tile_):
             return tile_[:].rearrange("k m c -> k (m c)").bitcast(F32)
 
-        for pair in range(PAIRS):
-            for part in range(2):
-                words = flat_words(q_tiles[pair][part])
-                for piece in range(GROUPS * P // 2 // BANK):
-                    nc.gpsimd.memset(words[:, BANK * piece : BANK * (piece + 1)], 0.0)
+        ZERO_WIDTH = 2 * BANK
+        zero_pieces = [
+            (pair, part, piece)
+            for pair in range(PAIRS)
+            for part in range(2)
+            for piece in range(GROUPS * P // 2 // ZERO_WIDTH)
+        ]
+
+        zeroed = [0]
+
+        def zero_q(count):
+            for z in range(count):
+                if zeroed[0] < len(zero_pieces):
+                    pair, part, piece = zero_pieces[zeroed[0]]
+                    zeroed[0] = zeroed[0] + 1
+                    words = flat_words(q_tiles[pair][part])
+                    nc.vector.memset(words[:, ZERO_WIDTH * piece : ZERO_WIDTH * (piece + 1)], 0.0)
+
+        zero_q(2)
 
         x_codes = keep.tile([P, TILES, PASSES * P], U32, align_bytes=64)
         x_planes = keep.tile([P, TILES, PASSES * P], U8, align_bytes=64)
@@ -158,6 +172,7 @@ def tile_differentialattention_pa_kernel(
         quantise(0)
         transpose_x(1)
         quantise(1)
+        zero_q(1)
 
         STEPS = PAIRS * CHUNKS
         acc_tiles = {}
@@ -338,6 +353,7 @@ def tile_differentialattention_pa_kernel(
             if i < STEPS:
                 split_hi(i, 1)
                 split_lo(i, 1)
+            zero_q(2 if i < 3 else 1)
             back(k)
             if 0 <= i - 1 < STEPS:
                 transpose_y(i - 1)

@@ -31,7 +31,7 @@ BANK = 512
 GROUPS = P // 2
 BATCH = BANK // (2 * ROWS)
 PAIR_BATCHES = GROUPS // BATCH
-FIRST_TICK_STEP = 11
+FIRST_TICK_STEP = 10
 RUN = 4
 
 SCALE = D ** -0.5
@@ -118,7 +118,7 @@ def tile_differentialattention_pa_kernel(
         ZERO_WIDTH = 2 * BANK
         zero_pieces = [
             (pair, part, piece)
-            for pair in range(PAIRS)
+            for pair in range(1)
             for part in range(2)
             for piece in range(GROUPS * P // 2 // ZERO_WIDTH)
         ]
@@ -173,6 +173,16 @@ def tile_differentialattention_pa_kernel(
         transpose_x(1)
         quantise(1)
         zero_q(1)
+
+        zeros = keep.tile([P, ZERO_WIDTH], F32)
+        nc.vector.memset(zeros[:], 0.0)
+        parked = out.rearrange("b (x n) a h -> (b x) (n a h)", x=P // TILES)
+        nc.sync.dma_start(out=parked, in_=zeros[:])
+        for part in range(2):
+            words = flat_words(q_tiles[1][part])
+            for piece in range(GROUPS * P // 2 // ZERO_WIDTH):
+                nc.sync.dma_start(out=words[:, ZERO_WIDTH * piece : ZERO_WIDTH * (piece + 1)], in_=parked)
+
 
         STEPS = PAIRS * CHUNKS
         acc_tiles = {}
@@ -353,7 +363,7 @@ def tile_differentialattention_pa_kernel(
             if i < STEPS:
                 split_hi(i, 1)
                 split_lo(i, 1)
-            zero_q(2 if i < 3 else 1)
+            zero_q(1)
             back(k)
             if 0 <= i - 1 < STEPS:
                 transpose_y(i - 1)
@@ -362,8 +372,8 @@ def tile_differentialattention_pa_kernel(
             if i == 9:
                 lam_value()
 
-        plain = keep.tile([P, 4 * H, H], F32)
-        result = keep.tile([P, 4 * H, H], F32)
+        plain = x_pool.tile([P, 4 * H, H], F32, tag="x_sb")
+        result = x_pool.tile([P, 4 * H, H], F32, tag="grouped", align_bytes=64)
         for quad in range(H // 4):
             heads = slice(4 * quad, 4 * (quad + 1))
             for j in range(2):

@@ -119,7 +119,7 @@ def tile_differentialattention_pa_kernel(
         zero_pieces = [
             (pair, part, piece)
             for pair in range(1)
-            for part in range(2)
+            for part in range(1)
             for piece in range(GROUPS * P // 2 // ZERO_WIDTH)
         ]
 
@@ -133,7 +133,22 @@ def tile_differentialattention_pa_kernel(
                     words = flat_words(q_tiles[pair][part])
                     nc.vector.memset(words[:, ZERO_WIDTH * piece : ZERO_WIDTH * (piece + 1)], 0.0)
 
-        zero_q(2)
+        few_zeros = keep.tile([P, 1, P], F32)
+        nc.vector.memset(few_zeros[:], 0.0)
+        copied = [0]
+
+        def zero_by_copy(count):
+            for z in range(count):
+                if copied[0] < GROUPS * P // 2 // ZERO_WIDTH:
+                    first = ZERO_WIDTH * copied[0]
+                    copied[0] = copied[0] + 1
+                    nc.scalar.copy(
+                        out=flat_words(q_tiles[0][1])[:, first : first + ZERO_WIDTH].rearrange("k (a b) -> k a b", b=P),
+                        in_=few_zeros[:].to_broadcast([P, ZERO_WIDTH // P, P]),
+                    )
+
+        zero_by_copy(2)
+        zero_q(1)
 
         x_codes = keep.tile([P, TILES, PASSES * P], U32, align_bytes=64)
         x_planes = keep.tile([P, TILES, PASSES * P], U8, align_bytes=64)
@@ -173,6 +188,7 @@ def tile_differentialattention_pa_kernel(
         transpose_x(1)
         quantise(1)
         zero_q(1)
+        zero_by_copy(1)
 
         zeros = keep.tile([P, ZERO_WIDTH], F32)
         nc.vector.memset(zeros[:], 0.0)
@@ -243,6 +259,8 @@ def tile_differentialattention_pa_kernel(
             for part in range(2):
                 copy = (nc.vector.tensor_copy, nc.scalar.copy)[part]
                 src = t_banks[i][part][:].rearrange("k (h c i) -> k c h i", h=CHUNK_HEADS, i=RUN)
+                if is_k(c) and pair == 0:
+                    copy = nc.scalar.copy
                 if is_k(c):
                     dst = flat_words(k_tiles[pair][part]).rearrange("k (c i x) -> k c x i", i=RUN, x=H)
                     copy(out=dst[:, :, h0 : h0 + CHUNK_HEADS, :], in_=src)
@@ -364,6 +382,7 @@ def tile_differentialattention_pa_kernel(
                 split_hi(i, 1)
                 split_lo(i, 1)
             zero_q(1)
+            zero_by_copy(1)
             back(k)
             if 0 <= i - 1 < STEPS:
                 transpose_y(i - 1)

@@ -309,6 +309,16 @@ def tile_differentialattention_pa_kernel(
         def exponentials(k):
             nc.scalar.activation(out=e_tiles[k][:], in_=e_tiles[k][:], func=ACT.Exp, scale=SCALE)
 
+        def keep_clock(k):
+            idle_bank = psum.tile([P, BANK], F32, tag="bank")
+            nc.tensor.matmul(
+                out=idle_bank[:, 0 : BATCH * ROWS],
+                lhsT=ident[:],
+                rhs=e_tiles[k][:].rearrange("q g r -> q (g r)"),
+                start=True,
+                stop=True,
+            )
+
         def add_up(k):
             total = soft.tile([P, BATCH], F32, tag="total")
             nc.vector.tensor_reduce(out=total[:], in_=e_tiles[k][:], axis=AXIS.X, op=ALU.add)
@@ -346,6 +356,8 @@ def tile_differentialattention_pa_kernel(
             def live(b):
                 return 0 <= b < BATCHES
 
+            if k == BATCHES:
+                keep_clock(k - 3)
             if live(k - 3):
                 add_up(k - 3)
             if live(k - 1):
@@ -358,6 +370,8 @@ def tile_differentialattention_pa_kernel(
                 subtract_max(k - 1)
             if live(k - 2):
                 exponentials(k - 2)
+                if k >= BATCHES:
+                    keep_clock(k - 2)
 
         def back(k):
             if 0 <= k < BATCHES:

@@ -48,7 +48,7 @@ def tile_differentialattention_pa_kernel(
         keep = ctx.enter_context(tc.tile_pool(name="keep", bufs=1))
         x_pool = ctx.enter_context(tc.tile_pool(name="x_pool", bufs=2))
         y_pool = ctx.enter_context(tc.tile_pool(name="y_pool", bufs=3))
-        soft = ctx.enter_context(tc.tile_pool(name="soft", bufs=6))
+        soft = ctx.enter_context(tc.tile_pool(name="soft", bufs=7))
         psum = ctx.enter_context(tc.psum_pool(name="psum", bufs=8))
         ctx.enter_context(tc.manual_schedule())
 
@@ -349,29 +349,26 @@ def tile_differentialattention_pa_kernel(
             nc.vector.tensor_tensor(out=neg_lam[:], in0=lam_exps[:, 1:2], in1=lam_exps[:, 0:1], op=ALU.subtract)
             nc.vector.tensor_scalar_add(out=neg_lam[:], in0=neg_lam[:], scalar1=-LAM_INIT)
 
-        LAG = 4
+        LAG = 5
         BATCHES = PAIRS * PAIR_BATCHES
 
         def front(k):
             def live(b):
                 return 0 <= b < BATCHES
 
-            if k == BATCHES:
-                keep_clock(k - 3)
-            if live(k - 3):
-                add_up(k - 3)
             if live(k - 1):
                 find_max(k - 1)
-            if live(k - 3):
-                invert(k - 3)
-            if live(k - 4):
-                normalise(k - 4)
-            if live(k - 1):
                 subtract_max(k - 1)
-            if live(k - 2):
-                exponentials(k - 2)
+            if live(k - 4):
+                add_up(k - 4)
+            if live(k - 5):
+                normalise(k - 5)
+            if live(k - 4):
+                invert(k - 4)
+            if live(k - 3):
+                exponentials(k - 3)
                 if k >= BATCHES:
-                    keep_clock(k - 2)
+                    keep_clock(k - 3)
 
         def back(k):
             if 0 <= k < BATCHES:

@@ -349,7 +349,7 @@ def tile_differentialattention_pa_kernel(
             nc.vector.tensor_tensor(out=neg_lam[:], in0=lam_exps[:, 1:2], in1=lam_exps[:, 0:1], op=ALU.subtract)
             nc.vector.tensor_scalar_add(out=neg_lam[:], in0=neg_lam[:], scalar1=-LAM_INIT)
 
-        LAG = 5
+        LAG = 6
         BATCHES = PAIRS * PAIR_BATCHES
 
         def front(k):
@@ -359,12 +359,12 @@ def tile_differentialattention_pa_kernel(
             if live(k - 1):
                 find_max(k - 1)
                 subtract_max(k - 1)
+            if live(k - 6):
+                normalise(k - 6)
+            if live(k - 5):
+                invert(k - 5)
             if live(k - 4):
                 add_up(k - 4)
-            if live(k - 5):
-                normalise(k - 5)
-            if live(k - 4):
-                invert(k - 4)
             if live(k - 3):
                 exponentials(k - 3)
                 if k >= BATCHES:

@@ -88,12 +88,14 @@ def tile_differentialattention_pa_kernel(
             chunk_words[c] = w
 
         load_x(0)
-        load_x(1)
         load_planes(1, Wk_scales)
+        load_planes(0, Wq_scales)
+        load_x(1)
         load_chunk(0, PASSES)
         load_chunk(1, PASSES)
-        load_planes(0, Wq_scales)
-        for c in range(2, 6):
+        load_chunk(2, 2)
+        load_chunk(3, 2)
+        for c in range(4, 6):
             load_chunk(c, 1)
         load_x(2)
         load_x(3)

@@ -55,13 +55,13 @@ def tile_differentialattention_pa_kernel(
         x_sb = {}
 
         def load_x(t):
-            x_tile = x_pool.tile([P, C], BF16, tag="x_sb")
+            x_tile = x_pool.tile([P, C], BF16, tag="x_sb", align_bytes=256)
             nc.sync.dma_start(out=x_tile[:], in_=x[t])
             x_sb[t] = x_tile
 
         w_planes = []
         for name in ("q", "k"):
-            planes = keep.tile([P, 2048], U8, name="w_planes_" + name, align_bytes=64)
+            planes = keep.tile([P, 2048], U8, name="w_planes_" + name, align_bytes=256)
             nc.vector.memset(planes[:].bitcast(I32), 0)
             w_planes.append(planes)
 
@@ -80,7 +80,7 @@ def tile_differentialattention_pa_kernel(
         def load_chunk(c, pieces):
             words = (Wq_words, Wk_words)[is_k(c)]
             first = 4 * CHUNK * (c % 4)
-            w = keep.tile([P, PASSES, 4 * CHUNK], U8, name="w%d" % c, align_bytes=64)
+            w = keep.tile([P, PASSES, 4 * CHUNK], U8, name="w%d" % c, align_bytes=256)
             src = words.rearrange("g p n t -> p g (n t)")[:, :, first : first + 4 * CHUNK]
             step = PASSES // pieces
             for g in range(0, PASSES, step):
@@ -105,14 +105,14 @@ def tile_differentialattention_pa_kernel(
         for v, vec in enumerate((lq1, lq2, lk1, lk2)):
             nc.sync.dma_start(out=lam_vecs[:, v, :], in_=vec.partition_broadcast(P))
 
-        ident = keep.tile([P, P], F32)
+        ident = keep.tile([P, P], F32, align_bytes=256)
         masks.make_identity(nc, ident[:])
         warm = keep.tile([P, 2], F32)
         nc.vector.memset(warm[:, 0:1], 0.0)
         nc.scalar.activation(out=warm[:, 1:2], in_=warm[:, 0:1], func=ACT.Exp)
 
-        q_tiles = [[keep.tile([P, GROUPS, P], BF16, name="q%d%d" % (pair, part)) for part in range(2)] for pair in range(PAIRS)]
-        k_tiles = [[keep.tile([P, GROUPS, 2 * ROWS], BF16, name="k%d%d" % (pair, part)) for part in range(2)] for pair in range(PAIRS)]
+        q_tiles = [[keep.tile([P, GROUPS, P], BF16, name="q%d%d" % (pair, part), align_bytes=256) for part in range(2)] for pair in range(PAIRS)]
+        k_tiles = [[keep.tile([P, GROUPS, 2 * ROWS], BF16, name="k%d%d" % (pair, part), align_bytes=256) for part in range(2)] for pair in range(PAIRS)]
 
         def flat_words(tile_):
             return tile_[:].rearrange("k m c -> k (m c)").bitcast(F32)
@@ -152,8 +152,8 @@ def tile_differentialattention_pa_kernel(
         zero_by_copy(2)
         zero_q(1)
 
-        x_codes = keep.tile([P, TILES, PASSES * P], U32, align_bytes=64)
-        x_planes = keep.tile([P, TILES, PASSES * P], U8, align_bytes=64)
+        x_codes = keep.tile([P, TILES, PASSES * P], U32, align_bytes=256)
+        x_planes = keep.tile([P, TILES, PASSES * P], U8, align_bytes=256)
         grouped_tiles = {}
 
         def quantise(t):
@@ -167,7 +167,7 @@ def tile_differentialattention_pa_kernel(
 
         def transpose_x(t):
             words = x_sb[t][:].bitcast(F32)
-            grouped = x_pool.tile([P, PASSES * P * 4], BF16, tag="grouped", align_bytes=64)
+            grouped = x_pool.tile([P, PASSES * P * 4], BF16, tag="grouped", align_bytes=256)
             grouped_tiles[t] = grouped
             grouped_words = grouped[:].bitcast(F32).rearrange("p (g n u) -> p g n u", g=PASSES, u=2)
             for half in range(2):
@@ -231,7 +231,7 @@ def tile_differentialattention_pa_kernel(
             acc_tiles[(i, s)] = acc
 
         def new_y(i):
-            y = y_pool.tile([P, 2, CHUNK_HEADS, 2, 2 * D], BF16, tag="y")
+            y = y_pool.tile([P, 2, CHUNK_HEADS, 2, 2 * D], BF16, tag="y", align_bytes=256)
             y_tiles[i] = y
 
         def split_hi(i, s):
@@ -273,7 +273,7 @@ def tile_differentialattention_pa_kernel(
                         first = H * s + h0
                         copy(out=dst[rows, :, first : first + CHUNK_HEADS, :], in_=src[rows, :, :, :])
 
-        w_all = keep.tile([P, ROWS, P], F32)
+        w_all = keep.tile([P, ROWS, P], F32, align_bytes=256)
         e_tiles, tops, totals, inverses = {}, {}, {}, {}
 
         def scores(k):
@@ -404,8 +404,8 @@ def tile_differentialattention_pa_kernel(
             if i == 9:
                 lam_value()
 
-        plain = x_pool.tile([P, 4 * H, H], F32, tag="x_sb")
-        result = x_pool.tile([P, 4 * H, H], F32, tag="grouped", align_bytes=64)
+        plain = x_pool.tile([P, 4 * H, H], F32, tag="x_sb", align_bytes=256)
+        result = x_pool.tile([P, 4 * H, H], F32, tag="grouped", align_bytes=256)
         for quad in range(H // 4):
             heads = slice(4 * quad, 4 * (quad + 1))
             for j in range(2):

@@ -88,13 +88,13 @@ def tile_differentialattention_pa_kernel(
             chunk_words[c] = w
 
         load_x(0)
-        load_planes(1, Wk_scales)
-        load_planes(0, Wq_scales)
         load_x(1)
+        load_planes(1, Wk_scales)
         load_chunk(0, PASSES)
         load_chunk(1, PASSES)
         load_chunk(2, 2)
         load_chunk(3, 2)
+        load_planes(0, Wq_scales)
         for c in range(4, 6):
             load_chunk(c, 1)
         load_x(2)
@@ -149,8 +149,8 @@ def tile_differentialattention_pa_kernel(
                         in_=few_zeros[:].to_broadcast([P, ZERO_WIDTH // P, P]),
                     )
 
-        zero_by_copy(2)
-        zero_q(1)
+        zero_by_copy(3)
+        zero_q(4)
 
         x_codes = keep.tile([P, TILES, PASSES * P], U32, align_bytes=256)
         x_planes = keep.tile([P, TILES, PASSES * P], U8, align_bytes=256)
@@ -189,7 +189,6 @@ def tile_differentialattention_pa_kernel(
         quantise(0)
         transpose_x(1)
         quantise(1)
-        zero_q(1)
         zero_by_copy(1)
 
         zeros = keep.tile([P, ZERO_WIDTH], F32)
@@ -211,16 +210,21 @@ def tile_differentialattention_pa_kernel(
             pair, place = divmod(i, CHUNKS)
             return pair, (place + 4 * pair) % CHUNKS
 
-        def project(i, s):
+        def project(i):
             pair, c = pair_chunk(i)
-            t = 2 * pair + s
             w = chunk_words[c]
             planes = w_planes[is_k(c)]
             cols = slice(CHUNK * (c % 4), CHUNK * (c % 4 + 1))
-            acc = psum.tile([P, BANK], F32, tag="bank")
-            for g in range(PASSES):
+            for s in range(2):
+                acc = psum.tile([P, BANK], F32, tag="bank")
+                acc_tiles[(i, s)] = acc
+            order = [(s, g) for s in range(2) for g in range(PASSES)]
+            if i < 3:
+                order = [(s, g) for g in range(PASSES) for s in range(2)]
+            for s, g in order:
+                t = 2 * pair + s
                 nc.tensor.matmul_mx(
-                    out=acc[:],
+                    out=acc_tiles[(i, s)][:],
                     lhsT=x_codes[:, t, P * g : P * (g + 1)].bitcast(FP8X4),
                     lhsT_scale=x_planes[:, t, P * g : P * (g + 1)],
                     rhs=w[:, g, :].bitcast(FP8X4),
@@ -228,7 +232,6 @@ def tile_differentialattention_pa_kernel(
                     start=(g == 0),
                     stop=(g == PASSES - 1),
                 )
-            acc_tiles[(i, s)] = acc
 
         def new_y(i):
             y = y_pool.tile([P, 2, CHUNK_HEADS, 2, 2 * D], BF16, tag="y", align_bytes=256)
@@ -381,8 +384,7 @@ def tile_differentialattention_pa_kernel(
             k = i - FIRST_TICK
             if i < STEPS:
                 new_y(i)
-                project(i, 0)
-                project(i, 1)
+                project(i)
             if 0 <= i - 2 < STEPS:
                 sort_rows(i - 2)
             front(k)
@@ -394,8 +396,6 @@ def tile_differentialattention_pa_kernel(
             if i < STEPS:
                 split_hi(i, 1)
                 split_lo(i, 1)
-            zero_q(1)
-            zero_by_copy(1)
             back(k)
             if 0 <= i - 1 < STEPS:
                 transpose_y(i - 1)

@@ -56,7 +56,7 @@ def tile_differentialattention_pa_kernel(
 
         def load_x(t):
             x_tile = x_pool.tile([P, C], BF16, tag="x_sb", align_bytes=256)
-            nc.sync.dma_start(out=x_tile[:], in_=x[t])
+            nc.sync.dma_start(out=x_tile[:], in_=x[t // 2 + PAIRS * (t % 2)])
             x_sb[t] = x_tile
 
         w_planes = []
@@ -191,10 +191,11 @@ def tile_differentialattention_pa_kernel(
         quantise(1)
         zero_by_copy(1)
 
-        zeros = keep.tile([P, ZERO_WIDTH], F32)
-        nc.vector.memset(zeros[:], 0.0)
+        w_all = keep.tile([P, ROWS, P], F32, align_bytes=256)
+        zeros = w_all[:, 0 : ZERO_WIDTH // P, :].rearrange("p c n -> p (c n)")
+        nc.vector.memset(zeros, 0.0)
         parked = out.rearrange("b (x n) a h -> (b x) (n a h)", x=P // TILES)
-        nc.sync.dma_start(out=parked, in_=zeros[:])
+        nc.sync.dma_start(out=parked, in_=zeros)
         for part in range(2):
             words = flat_words(q_tiles[1][part])
             for piece in range(GROUPS * P // 2 // ZERO_WIDTH):
@@ -276,11 +277,14 @@ def tile_differentialattention_pa_kernel(
                         first = H * s + h0
                         copy(out=dst[rows, :, first : first + CHUNK_HEADS, :], in_=src[rows, :, :, :])
 
-        w_all = keep.tile([P, ROWS, P], F32, align_bytes=256)
+        BATCHES = PAIRS * PAIR_BATCHES
+        units = [(b, 2) for b in range(0, BATCHES, 2)]
+        unit_of = {first + place: (first, count) for first, count in units for place in range(count)}
         e_tiles, tops, totals, inverses = {}, {}, {}, {}
 
         def scores(k):
             pair, b = divmod(k, PAIR_BATCHES)
+            first, count = unit_of[k]
             bank = psum.tile([P, BANK], F32, tag="bank")
             for g in range(BATCH):
                 m = BATCH * b + g
@@ -293,52 +297,57 @@ def tile_differentialattention_pa_kernel(
                         start=(term == 0),
                         stop=(term == len(terms) - 1),
                     )
-            e = soft.tile([P, BATCH, ROWS], F32, tag="e")
+            if k == first:
+                e = soft.tile([P, count * BATCH, ROWS], F32, tag="e", bufs=6)
+                e_tiles[first] = e
+            own = slice(BATCH * (k - first), BATCH * (k - first + 1))
             sc = bank[:].rearrange("q (g u r) -> q g u r", u=2, r=ROWS)
             for u in range(2):
                 rows = slice(64 * u, 64 * (u + 1))
-                nc.scalar.copy(out=e[rows, :, :], in_=sc[rows, :, u, :])
-            e_tiles[k] = e
+                nc.scalar.copy(out=e_tiles[first][rows, own, :], in_=sc[rows, :, u, :])
+
+        def values(k):
+            first, count = unit_of[k]
+            return e_tiles[first][:, BATCH * (k - first) : BATCH * (k - first + 1), :]
 
         def find_max(k):
             top = soft.tile([P, BATCH], F32, tag="top")
-            nc.vector.tensor_reduce(out=top[:], in_=e_tiles[k][:], axis=AXIS.X, op=ALU.max)
+            nc.vector.tensor_reduce(out=top[:], in_=values(k), axis=AXIS.X, op=ALU.max)
             tops[k] = top
 
         def subtract_max(k):
-            e = e_tiles[k]
             nc.gpsimd.tensor_tensor(
-                out=e[:], in0=e[:], in1=tops[k][:].unsqueeze(2).to_broadcast([P, BATCH, ROWS]), op=ALU.subtract
+                out=values(k), in0=values(k), in1=tops[k][:].unsqueeze(2).to_broadcast([P, BATCH, ROWS]), op=ALU.subtract
             )
 
         def exponentials(k):
-            nc.scalar.activation(out=e_tiles[k][:], in_=e_tiles[k][:], func=ACT.Exp, scale=SCALE)
+            nc.scalar.activation(out=values(k), in_=values(k), func=ACT.Exp, scale=SCALE)
 
         def keep_clock(k):
             idle_bank = psum.tile([P, BANK], F32, tag="bank")
             nc.tensor.matmul(
                 out=idle_bank[:, 0 : BATCH * ROWS],
                 lhsT=ident[:],
-                rhs=e_tiles[k][:].rearrange("q g r -> q (g r)"),
+                rhs=values(k).rearrange("q g r -> q (g r)"),
                 start=True,
                 stop=True,
             )
 
-        def add_up(k):
-            total = soft.tile([P, BATCH], F32, tag="total")
-            nc.vector.tensor_reduce(out=total[:], in_=e_tiles[k][:], axis=AXIS.X, op=ALU.add)
-            totals[k] = total
+        def add_up(first, n):
+            total = soft.tile([P, n], F32, tag="total")
+            nc.vector.tensor_reduce(out=total[:], in_=e_tiles[first][:], axis=AXIS.X, op=ALU.add)
+            totals[first] = total
 
-        def invert(k):
-            inverse = soft.tile([P, BATCH], F32, tag="inverse")
-            nc.vector.reciprocal(out=inverse[:], in_=totals[k][:])
-            inverses[k] = inverse
+        def invert(first, n):
+            inverse = soft.tile([P, n], F32, tag="inverse")
+            nc.vector.reciprocal(out=inverse[:], in_=totals[first][:])
+            inverses[first] = inverse
 
-        def normalise(k):
+        def normalise(first, n):
             nc.vector.tensor_tensor(
-                out=w_all[:, :, BATCH * k : BATCH * (k + 1)].rearrange("q (c i) g -> q c g i", i=RUN),
-                in0=e_tiles[k][:].rearrange("q g (c i) -> q c g i", i=RUN),
-                in1=inverses[k][:].unsqueeze(1).unsqueeze(3).to_broadcast([P, ROWS // RUN, BATCH, RUN]),
+                out=w_all[:, :, BATCH * first : BATCH * first + n].rearrange("q (c i) g -> q c g i", i=RUN),
+                in0=e_tiles[first][:].rearrange("q g (c i) -> q c g i", i=RUN),
+                in1=inverses[first][:].unsqueeze(1).unsqueeze(3).to_broadcast([P, ROWS // RUN, n, RUN]),
                 op=ALU.mult,
             )
 
@@ -354,23 +363,26 @@ def tile_differentialattention_pa_kernel(
             nc.vector.tensor_tensor(out=neg_lam[:], in0=lam_exps[:, 1:2], in1=lam_exps[:, 0:1], op=ALU.subtract)
             nc.vector.tensor_scalar_add(out=neg_lam[:], in0=neg_lam[:], scalar1=-LAM_INIT)
 
-        LAG = 6
-        BATCHES = PAIRS * PAIR_BATCHES
+        LAG = 7
 
         def front(k):
-            def live(b):
-                return 0 <= b < BATCHES
+            def live(lag):
+                return 0 <= k - lag < BATCHES
 
-            if live(k - 1):
+            def unit(lag):
+                first, count = unit_of.get(k - lag, (None, 0))
+                return (first, BATCH * count) if first is not None and k - lag == first + count - 1 else None
+
+            if live(1):
                 find_max(k - 1)
                 subtract_max(k - 1)
-            if live(k - 6):
-                normalise(k - 6)
-            if live(k - 5):
-                invert(k - 5)
-            if live(k - 4):
-                add_up(k - 4)
-            if live(k - 3):
+            if unit(7):
+                normalise(*unit(7))
+            if unit(5):
+                invert(*unit(5))
+            if unit(4):
+                add_up(*unit(4))
+            if live(3):
                 exponentials(k - 3)
                 if k >= BATCHES:
                     keep_clock(k - 3)
@@ -421,12 +433,7 @@ def tile_differentialattention_pa_kernel(
                         out=result[:, :, heads], in0=own, scalar=neg_lam[:, 0:1], in1=plain[:, :, heads],
                         op0=ALU.mult, op1=ALU.add,
                     )
-        out_view = out.rearrange("(w s) (m u) a h -> w u m s (a h)", s=2, u=2)
-        for pair in range(PAIRS):
-            for u in range(2):
-                nc.sync.dma_start(
-                    out=out_view[pair, u],
-                    in_=result[GROUPS * pair : GROUPS * (pair + 1), 2 * H * u : 2 * H * (u + 1), :].rearrange(
-                        "m (s a) h -> m s (a h)", s=2
-                    ),
-                )
+        out_view = out.rearrange("(s w) (m u) a h -> s (w m) u (a h)", s=2, u=2)
+        halves = result[:].rearrange("p (u s a) h -> p s u (a h)", u=2, s=2)
+        for s in range(2):
+            nc.sync.dma_start(out=out_view[s], in_=halves[:, s, :, :])

@@ -278,37 +278,36 @@ def tile_differentialattention_pa_kernel(
                         copy(out=dst[rows, :, first : first + CHUNK_HEADS, :], in_=src[rows, :, :, :])
 
         BATCHES = PAIRS * PAIR_BATCHES
-        units = [(b, 2) for b in range(0, BATCHES, 2)]
-        unit_of = {first + place: (first, count) for first, count in units for place in range(count)}
         e_tiles, tops, totals, inverses = {}, {}, {}, {}
 
         def scores(k):
             pair, b = divmod(k, PAIR_BATCHES)
-            first, count = unit_of[k]
-            bank = psum.tile([P, BANK], F32, tag="bank")
+            banks = []
+            for place in range(2):
+                bank = psum.tile([P, BANK], F32, tag="bank")
+                banks.append(bank)
+            terms = ((0, 0), (0, 1), (1, 0))
             for g in range(BATCH):
-                m = BATCH * b + g
-                terms = ((0, 0), (0, 1), (1, 0))
                 for term, (q_part, k_part) in enumerate(terms):
-                    nc.tensor.matmul(
-                        out=bank[:, 2 * ROWS * g : 2 * ROWS * (g + 1)],
-                        lhsT=q_tiles[pair][q_part][:, m, :],
-                        rhs=k_tiles[pair][k_part][:, m, :],
-                        start=(term == 0),
-                        stop=(term == len(terms) - 1),
-                    )
-            if k == first:
-                e = soft.tile([P, count * BATCH, ROWS], F32, tag="e", bufs=6)
-                e_tiles[first] = e
-            own = slice(BATCH * (k - first), BATCH * (k - first + 1))
-            sc = bank[:].rearrange("q (g u r) -> q g u r", u=2, r=ROWS)
-            for u in range(2):
-                rows = slice(64 * u, 64 * (u + 1))
-                nc.scalar.copy(out=e_tiles[first][rows, own, :], in_=sc[rows, :, u, :])
+                    for place in range(2):
+                        m = BATCH * (b + place) + g
+                        nc.tensor.matmul(
+                            out=banks[place][:, 2 * ROWS * g : 2 * ROWS * (g + 1)],
+                            lhsT=q_tiles[pair][q_part][:, m, :],
+                            rhs=k_tiles[pair][k_part][:, m, :],
+                            start=(term == 0),
+                            stop=(term == len(terms) - 1),
+                        )
+            e = soft.tile([P, 2 * BATCH, ROWS], F32, tag="e", bufs=6)
+            e_tiles[k] = e
+            for place in range(2):
+                sc = banks[place][:].rearrange("q (g u r) -> q g u r", u=2, r=ROWS)
+                for u in range(2):
+                    rows = slice(64 * u, 64 * (u + 1))
+                    nc.scalar.copy(out=e[rows, BATCH * place : BATCH * (place + 1), :], in_=sc[rows, :, u, :])
 
         def values(k):
-            first, count = unit_of[k]
-            return e_tiles[first][:, BATCH * (k - first) : BATCH * (k - first + 1), :]
+            return e_tiles[k - k % 2][:, BATCH * (k % 2) : BATCH * (k % 2 + 1), :]
 
         def find_max(k):
             top = soft.tile([P, BATCH], F32, tag="top")
@@ -363,33 +362,32 @@ def tile_differentialattention_pa_kernel(
             nc.vector.tensor_tensor(out=neg_lam[:], in0=lam_exps[:, 1:2], in1=lam_exps[:, 0:1], op=ALU.subtract)
             nc.vector.tensor_scalar_add(out=neg_lam[:], in0=neg_lam[:], scalar1=-LAM_INIT)
 
-        LAG = 7
+        LAG = 8
 
         def front(k):
             def live(lag):
                 return 0 <= k - lag < BATCHES
 
-            def unit(lag):
-                first, count = unit_of.get(k - lag, (None, 0))
-                return (first, BATCH * count) if first is not None and k - lag == first + count - 1 else None
+            def second(lag):
+                return live(lag) and (k - lag) % 2 == 1
 
-            if live(1):
-                find_max(k - 1)
-                subtract_max(k - 1)
-            if unit(7):
-                normalise(*unit(7))
-            if unit(5):
-                invert(*unit(5))
-            if unit(4):
-                add_up(*unit(4))
-            if live(3):
-                exponentials(k - 3)
+            if live(2):
+                find_max(k - 2)
+                subtract_max(k - 2)
+            if second(8):
+                normalise(k - 8 - 1, 2 * BATCH)
+            if second(6):
+                invert(k - 6 - 1, 2 * BATCH)
+            if second(5):
+                add_up(k - 5 - 1, 2 * BATCH)
+            if live(4):
+                exponentials(k - 4)
                 if k >= BATCHES:
-                    keep_clock(k - 3)
+                    keep_clock(k - 4)
 
         def back(k):
-            if 0 <= k < BATCHES:
-                scores(k)
+            if 0 <= k < BATCHES and k % 2 == 1:
+                scores(k - 1)
 
         FIRST_TICK = FIRST_TICK_STEP
         for i in range(FIRST_TICK + BATCHES + LAG):
@@ -408,9 +406,12 @@ def tile_differentialattention_pa_kernel(
             if i < STEPS:
                 split_hi(i, 1)
                 split_lo(i, 1)
-            back(k)
+            if i < STEPS:
+                back(k)
             if 0 <= i - 1 < STEPS:
                 transpose_y(i - 1)
+            if i >= STEPS:
+                back(k)
             if i in (5, 6):
                 transpose_x(i - 3)
             if i == 9:

@@ -165,10 +165,23 @@ def tile_differentialattention_pa_kernel(
                     in_=grouped_tiles[t][:, 8 * P * half : 8 * P * (half + 1)],
                 )
 
-        def transpose_x(t):
-            words = x_sb[t][:].bitcast(F32)
+        def order_words(t):
             grouped = x_pool.tile([P, PASSES * P * 4], BF16, tag="grouped", align_bytes=256)
+            nc.vector.tensor_copy(
+                out=grouped[:].bitcast(F32).rearrange("n (g u p) -> n g u p", g=PASSES, u=2),
+                in_=x_sb[t][:].bitcast(F32).rearrange("n (g p u) -> n g u p", g=PASSES, u=2),
+            )
             grouped_tiles[t] = grouped
+
+        def transpose_x(t):
+            ordered = t in grouped_tiles
+            if ordered:
+                grouped = grouped_tiles[t]
+                words = grouped[:].bitcast(F32)
+            else:
+                grouped = x_pool.tile([P, PASSES * P * 4], BF16, tag="grouped", align_bytes=256)
+                grouped_tiles[t] = grouped
+                words = x_sb[t][:].bitcast(F32)
             grouped_words = grouped[:].bitcast(F32).rearrange("p (g n u) -> p g n u", g=PASSES, u=2)
             for half in range(2):
                 bank = psum.tile([P, BANK], F32, tag="bank")
@@ -176,9 +189,11 @@ def tile_differentialattention_pa_kernel(
                 for gg in range(2):
                     g = 2 * half + gg
                     for u in range(2):
-                        nc.tensor.transpose(
-                            planes[:, gg, u, :], words[:, 256 * g + u : 256 * (g + 1) : 2], ident[:]
-                        )
+                        if ordered:
+                            own = words[:, 256 * g + P * u : 256 * g + P * (u + 1)]
+                        else:
+                            own = words[:, 256 * g + u : 256 * (g + 1) : 2]
+                        nc.tensor.transpose(planes[:, gg, u, :], own, ident[:])
                 copy = (nc.vector.tensor_copy, nc.scalar.copy)[half]
                 copy(
                     out=grouped_words[:, 2 * half : 2 * half + 2, :, :],
@@ -280,16 +295,16 @@ def tile_differentialattention_pa_kernel(
         BATCHES = PAIRS * PAIR_BATCHES
         e_tiles, tops, totals, inverses = {}, {}, {}, {}
 
-        def scores(k):
+        def scores(k, count):
             pair, b = divmod(k, PAIR_BATCHES)
             banks = []
-            for place in range(2):
+            for place in range(count):
                 bank = psum.tile([P, BANK], F32, tag="bank")
                 banks.append(bank)
             terms = ((0, 0), (0, 1), (1, 0))
             for g in range(BATCH):
                 for term, (q_part, k_part) in enumerate(terms):
-                    for place in range(2):
+                    for place in range(count):
                         m = BATCH * (b + place) + g
                         nc.tensor.matmul(
                             out=banks[place][:, 2 * ROWS * g : 2 * ROWS * (g + 1)],
@@ -298,13 +313,15 @@ def tile_differentialattention_pa_kernel(
                             start=(term == 0),
                             stop=(term == len(terms) - 1),
                         )
-            e = soft.tile([P, 2 * BATCH, ROWS], F32, tag="e", bufs=6)
-            e_tiles[k] = e
-            for place in range(2):
+            if k % 2 == 0:
+                e = soft.tile([P, 2 * BATCH, ROWS], F32, tag="e", bufs=6)
+                e_tiles[k] = e
+            for place in range(count):
                 sc = banks[place][:].rearrange("q (g u r) -> q g u r", u=2, r=ROWS)
+                own = values(k + place)
                 for u in range(2):
                     rows = slice(64 * u, 64 * (u + 1))
-                    nc.scalar.copy(out=e[rows, BATCH * place : BATCH * (place + 1), :], in_=sc[rows, :, u, :])
+                    nc.scalar.copy(out=own[rows, :, :], in_=sc[rows, :, u, :])
 
         def values(k):
             return e_tiles[k - k % 2][:, BATCH * (k % 2) : BATCH * (k % 2 + 1), :]
@@ -382,12 +399,14 @@ def tile_differentialattention_pa_kernel(
                 add_up(k - 5 - 1, 2 * BATCH)
             if live(4):
                 exponentials(k - 4)
-                if k >= BATCHES:
+                if k - 4 >= BATCHES - 3:
                     keep_clock(k - 4)
 
         def back(k):
-            if 0 <= k < BATCHES and k % 2 == 1:
-                scores(k - 1)
+            if 0 <= k < 14 and k % 2 == 1:
+                scores(k - 1, 2)
+            if 14 <= k < BATCHES:
+                scores(k, 1)
 
         FIRST_TICK = FIRST_TICK_STEP
         for i in range(FIRST_TICK + BATCHES + LAG):
@@ -395,6 +414,8 @@ def tile_differentialattention_pa_kernel(
             if i < STEPS:
                 new_y(i)
                 project(i)
+            if i in (5, 6):
+                order_words(i - 3)
             if 0 <= i - 2 < STEPS:
                 sort_rows(i - 2)
             front(k)

from contextlib import ExitStack

import math

import concourse.masks as masks
import concourse.mybir as mybir

F32 = mybir.dt.float32
BF16 = mybir.dt.bfloat16
I32 = mybir.dt.int32
U8 = mybir.dt.uint8
U32 = mybir.dt.uint32
FP8X4 = mybir.dt.float8_e4m3fn_x4
ALU = mybir.AluOpType
ACT = mybir.ActivationFunctionType
AXIS = mybir.AxisListType

P = 128
TILES = 4
PAIRS = TILES // 2
C = 2048
K_PASS = 512
PASSES = C // K_PASS
CHUNK = 512
CHUNKS = 2 * 2048 // CHUNK
H = 16
D = 64
ROWS = 2 * H
CHUNK_HEADS = CHUNK // (2 * D)
BANK = 512
GROUPS = P // 2
BATCH = BANK // (2 * ROWS)
PAIR_BATCHES = GROUPS // BATCH
FIRST_TICK_STEP = 10
RUN = 4

SCALE = D ** -0.5
LAM_INIT = 0.8 - 0.6 * math.exp(-0.3 * 12)

FLOPS = 2 * TILES * P * C * 2 * 2048 + 2 * TILES * P * ROWS * ROWS * D


def tile_differentialattention_pa_kernel(
    tc, x, Wq_words, Wq_scales, Wk_words, Wk_scales, lq1, lq2, lk1, lk2, out
):
    nc = tc.nc
    with ExitStack() as ctx:
        keep = ctx.enter_context(tc.tile_pool(name="keep", bufs=1))
        x_pool = ctx.enter_context(tc.tile_pool(name="x_pool", bufs=2))
        y_pool = ctx.enter_context(tc.tile_pool(name="y_pool", bufs=3))
        soft = ctx.enter_context(tc.tile_pool(name="soft", bufs=7))
        psum = ctx.enter_context(tc.psum_pool(name="psum", bufs=8))
        ctx.enter_context(tc.manual_schedule())

        x_sb = {}

        def load_x(t):
            x_tile = x_pool.tile([P, C], BF16, tag="x_sb", align_bytes=256)
            nc.sync.dma_start(out=x_tile[:], in_=x[t // 2 + PAIRS * (t % 2)])
            x_sb[t] = x_tile

        w_planes = []
        for name in ("q", "k"):
            planes = keep.tile([P, 2048], U8, name="w_planes_" + name, align_bytes=256)
            nc.vector.memset(planes[:].bitcast(I32), 0)
            w_planes.append(planes)

        def load_planes(which, scales):
            for quad in range(4):
                nc.sync.dma_start(
                    out=w_planes[which][32 * quad : 32 * quad + 16, :].bitcast(I32),
                    in_=scales[:, 4 * quad : 4 * quad + 4, :].bitcast(I32),
                )

        chunk_words = {}

        def is_k(c):
            return 1 if c < 4 else 0

        def load_chunk(c, pieces):
            words = (Wq_words, Wk_words)[is_k(c)]
            first = 4 * CHUNK * (c % 4)
            w = keep.tile([P, PASSES, 4 * CHUNK], U8, name="w%d" % c, align_bytes=256)
            src = words.rearrange("g p n t -> p g (n t)")[:, :, first : first + 4 * CHUNK]
            step = PASSES // pieces
            for g in range(0, PASSES, step):
                nc.sync.dma_start(out=w[:, g : g + step, :].bitcast(I32), in_=src[:, g : g + step, :].bitcast(I32))
            chunk_words[c] = w

        load_x(0)
        load_x(1)
        load_planes(1, Wk_scales)
        load_chunk(0, PASSES)
        load_chunk(1, PASSES)
        load_chunk(2, 2)
        load_chunk(3, 2)
        load_planes(0, Wq_scales)
        for c in range(4, 6):
            load_chunk(c, 1)
        load_x(2)
        load_x(3)
        for c in range(6, CHUNKS):
            load_chunk(c, 1)
        lam_vecs = keep.tile([P, 4, D], BF16)
        for v, vec in enumerate((lq1, lq2, lk1, lk2)):
            nc.sync.dma_start(out=lam_vecs[:, v, :], in_=vec.partition_broadcast(P))

        ident = keep.tile([P, P], F32, align_bytes=256)
        masks.make_identity(nc, ident[:])
        warm = keep.tile([P, 2], F32)
        nc.vector.memset(warm[:, 0:1], 0.0)
        nc.scalar.activation(out=warm[:, 1:2], in_=warm[:, 0:1], func=ACT.Exp)

        q_tiles = [[keep.tile([P, GROUPS, P], BF16, name="q%d%d" % (pair, part), align_bytes=256) for part in range(2)] for pair in range(PAIRS)]
        k_tiles = [[keep.tile([P, GROUPS, 2 * ROWS], BF16, name="k%d%d" % (pair, part), align_bytes=256) for part in range(2)] for pair in range(PAIRS)]

        def flat_words(tile_):
            return tile_[:].rearrange("k m c -> k (m c)").bitcast(F32)

        ZERO_WIDTH = 2 * BANK
        zero_pieces = [
            (pair, part, piece)
            for pair in range(1)
            for part in range(1)
            for piece in range(GROUPS * P // 2 // ZERO_WIDTH)
        ]

        zeroed = [0]

        def zero_q(count):
            for z in range(count):
                if zeroed[0] < len(zero_pieces):
                    pair, part, piece = zero_pieces[zeroed[0]]
                    zeroed[0] = zeroed[0] + 1
                    words = flat_words(q_tiles[pair][part])
                    nc.vector.memset(words[:, ZERO_WIDTH * piece : ZERO_WIDTH * (piece + 1)], 0.0)

        few_zeros = keep.tile([P, 1, P], F32)
        nc.vector.memset(few_zeros[:], 0.0)
        copied = [0]

        def zero_by_copy(count):
            for z in range(count):
                if copied[0] < GROUPS * P // 2 // ZERO_WIDTH:
                    first = ZERO_WIDTH * copied[0]
                    copied[0] = copied[0] + 1
                    nc.scalar.copy(
                        out=flat_words(q_tiles[0][1])[:, first : first + ZERO_WIDTH].rearrange("k (a b) -> k a b", b=P),
                        in_=few_zeros[:].to_broadcast([P, ZERO_WIDTH // P, P]),
                    )

        zero_by_copy(3)
        zero_q(4)

        x_codes = keep.tile([P, TILES, PASSES * P], U32, align_bytes=256)
        x_planes = keep.tile([P, TILES, PASSES * P], U8, align_bytes=256)
        grouped_tiles = {}

        def quantise(t):
            for half in range(2):
                cols = slice(2 * P * half, 2 * P * (half + 1))
                nc.vector.quantize_mx(
                    out=x_codes[:, t, cols].bitcast(FP8X4),
                    scales=x_planes[:, t, cols],
                    in_=grouped_tiles[t][:, 8 * P * half : 8 * P * (half + 1)],
                )

        def order_words(t):
            grouped = x_pool.tile([P, PASSES * P * 4], BF16, tag="grouped", align_bytes=256)
            nc.vector.tensor_copy(
                out=grouped[:].bitcast(F32).rearrange("n (g u p) -> n g u p", g=PASSES, u=2),
                in_=x_sb[t][:].bitcast(F32).rearrange("n (g p u) -> n g u p", g=PASSES, u=2),
            )
            grouped_tiles[t] = grouped

        def transpose_x(t):
            ordered = t in grouped_tiles
            if ordered:
                grouped = grouped_tiles[t]
                words = grouped[:].bitcast(F32)
            else:
                grouped = x_pool.tile([P, PASSES * P * 4], BF16, tag="grouped", align_bytes=256)
                grouped_tiles[t] = grouped
                words = x_sb[t][:].bitcast(F32)
            grouped_words = grouped[:].bitcast(F32).rearrange("p (g n u) -> p g n u", g=PASSES, u=2)
            for half in range(2):
                bank = psum.tile([P, BANK], F32, tag="bank")
                planes = bank[:].rearrange("p (g u n) -> p g u n", g=2, u=2)
                for gg in range(2):
                    g = 2 * half + gg
                    for u in range(2):
                        if ordered:
                            own = words[:, 256 * g + P * u : 256 * g + P * (u + 1)]
                        else:
                            own = words[:, 256 * g + u : 256 * (g + 1) : 2]
                        nc.tensor.transpose(planes[:, gg, u, :], own, ident[:])
                copy = (nc.vector.tensor_copy, nc.scalar.copy)[half]
                copy(
                    out=grouped_words[:, 2 * half : 2 * half + 2, :, :],
                    in_=planes.rearrange("p g u n -> p g n u"),
                )

        transpose_x(0)
        quantise(0)
        transpose_x(1)
        quantise(1)
        zero_by_copy(1)

        w_all = keep.tile([P, ROWS, P], F32, align_bytes=256)
        zeros = w_all[:, 0 : ZERO_WIDTH // P, :].rearrange("p c n -> p (c n)")
        nc.vector.memset(zeros, 0.0)
        parked = out.rearrange("b (x n) a h -> (b x) (n a h)", x=P // TILES)
        nc.sync.dma_start(out=parked, in_=zeros)
        for part in range(2):
            words = flat_words(q_tiles[1][part])
            for piece in range(GROUPS * P // 2 // ZERO_WIDTH):
                nc.sync.dma_start(out=words[:, ZERO_WIDTH * piece : ZERO_WIDTH * (piece + 1)], in_=parked)


        STEPS = PAIRS * CHUNKS
        acc_tiles = {}
        y_tiles = {}
        t_banks = {}

        def pair_chunk(i):
            pair, place = divmod(i, CHUNKS)
            return pair, (place + 4 * pair) % CHUNKS

        def project(i):
            pair, c = pair_chunk(i)
            w = chunk_words[c]
            planes = w_planes[is_k(c)]
            cols = slice(CHUNK * (c % 4), CHUNK * (c % 4 + 1))
            for s in range(2):
                acc = psum.tile([P, BANK], F32, tag="bank")
                acc_tiles[(i, s)] = acc
            order = [(s, g) for s in range(2) for g in range(PASSES)]
            if i < 3:
                order = [(s, g) for g in range(PASSES) for s in range(2)]
            for s, g in order:
                t = 2 * pair + s
                nc.tensor.matmul_mx(
                    out=acc_tiles[(i, s)][:],
                    lhsT=x_codes[:, t, P * g : P * (g + 1)].bitcast(FP8X4),
                    lhsT_scale=x_planes[:, t, P * g : P * (g + 1)],
                    rhs=w[:, g, :].bitcast(FP8X4),
                    rhs_scale=planes[4 * g : P, cols],
                    start=(g == 0),
                    stop=(g == PASSES - 1),
                )

        def new_y(i):
            y = y_pool.tile([P, 2, CHUNK_HEADS, 2, 2 * D], BF16, tag="y", align_bytes=256)
            y_tiles[i] = y

        def split_hi(i, s):
            by_head = acc_tiles[(i, s)][:].rearrange("p (h e) -> p h e", h=CHUNK_HEADS)
            nc.scalar.copy(out=y_tiles[i][:, 0, :, s, :], in_=by_head)

        def split_lo(i, s):
            by_head = acc_tiles[(i, s)][:].rearrange("p (h e) -> p h e", h=CHUNK_HEADS)
            nc.vector.tensor_tensor(
                out=y_tiles[i][:, 1, :, s, :], in0=by_head, in1=y_tiles[i][:, 0, :, s, :], op=ALU.subtract
            )

        def transpose_y(i):
            y = y_tiles[i]
            banks = []
            for part in range(2):
                bank = psum.tile([P, BANK], F32, tag="bank")
                for h in range(CHUNK_HEADS):
                    words = y[:, part, h, :, :].rearrange("p s e -> p (s e)").bitcast(F32)
                    nc.tensor.transpose(bank[:, P * h : P * (h + 1)], words, ident[:])
                banks.append(bank)
            t_banks[i] = banks

        def sort_rows(i):
            pair, c = pair_chunk(i)
            h0 = CHUNK_HEADS * (c % 4)
            for part in range(2):
                copy = (nc.vector.tensor_copy, nc.scalar.copy)[part]
                src = t_banks[i][part][:].rearrange("k (h c i) -> k c h i", h=CHUNK_HEADS, i=RUN)
                if is_k(c) and pair == 0:
                    copy = nc.scalar.copy
                if is_k(c):
                    dst = flat_words(k_tiles[pair][part]).rearrange("k (c i x) -> k c x i", i=RUN, x=H)
                    copy(out=dst[:, :, h0 : h0 + CHUNK_HEADS, :], in_=src)
                else:
                    dst = flat_words(q_tiles[pair][part]).rearrange("k (c i x) -> k c x i", i=RUN, x=2 * H)
                    for s in range(2):
                        rows = slice(D * s, D * (s + 1))
                        first = H * s + h0
                        copy(out=dst[rows, :, first : first + CHUNK_HEADS, :], in_=src[rows, :, :, :])

        BATCHES = PAIRS * PAIR_BATCHES
        e_tiles, tops, totals, inverses = {}, {}, {}, {}

        def scores(k, count):
            pair, b = divmod(k, PAIR_BATCHES)
            banks = []
            for place in range(count):
                bank = psum.tile([P, BANK], F32, tag="bank")
                banks.append(bank)
            terms = ((0, 0), (0, 1), (1, 0))
            for g in range(BATCH):
                for term, (q_part, k_part) in enumerate(terms):
                    for place in range(count):
                        m = BATCH * (b + place) + g
                        nc.tensor.matmul(
                            out=banks[place][:, 2 * ROWS * g : 2 * ROWS * (g + 1)],
                            lhsT=q_tiles[pair][q_part][:, m, :],
                            rhs=k_tiles[pair][k_part][:, m, :],
                            start=(term == 0),
                            stop=(term == len(terms) - 1),
                        )
            if k % 2 == 0:
                e = soft.tile([P, 2 * BATCH, ROWS], F32, tag="e", bufs=6)
                e_tiles[k] = e
            for place in range(count):
                sc = banks[place][:].rearrange("q (g u r) -> q g u r", u=2, r=ROWS)
                own = values(k + place)
                for u in range(2):
                    rows = slice(64 * u, 64 * (u + 1))
                    nc.scalar.copy(out=own[rows, :, :], in_=sc[rows, :, u, :])

        def values(k):
            return e_tiles[k - k % 2][:, BATCH * (k % 2) : BATCH * (k % 2 + 1), :]

        def find_max(k):
            top = soft.tile([P, BATCH], F32, tag="top")
            nc.vector.tensor_reduce(out=top[:], in_=values(k), axis=AXIS.X, op=ALU.max)
            tops[k] = top

        def subtract_max(k):
            nc.gpsimd.tensor_tensor(
                out=values(k), in0=values(k), in1=tops[k][:].unsqueeze(2).to_broadcast([P, BATCH, ROWS]), op=ALU.subtract
            )

        def exponentials(k):
            nc.scalar.activation(out=values(k), in_=values(k), func=ACT.Exp, scale=SCALE)

        def keep_clock(k):
            idle_bank = psum.tile([P, BANK], F32, tag="bank")
            nc.tensor.matmul(
                out=idle_bank[:, 0 : BATCH * ROWS],
                lhsT=ident[:],
                rhs=values(k).rearrange("q g r -> q (g r)"),
                start=True,
                stop=True,
            )

        def add_up(first, n):
            total = soft.tile([P, n], F32, tag="total")
            nc.vector.tensor_reduce(out=total[:], in_=e_tiles[first][:], axis=AXIS.X, op=ALU.add)
            totals[first] = total

        def invert(first, n):
            inverse = soft.tile([P, n], F32, tag="inverse")
            nc.vector.reciprocal(out=inverse[:], in_=totals[first][:])
            inverses[first] = inverse

        def normalise(first, n):
            nc.vector.tensor_tensor(
                out=w_all[:, :, BATCH * first : BATCH * first + n].rearrange("q (c i) g -> q c g i", i=RUN),
                in0=e_tiles[first][:].rearrange("q g (c i) -> q c g i", i=RUN),
                in1=inverses[first][:].unsqueeze(1).unsqueeze(3).to_broadcast([P, ROWS // RUN, n, RUN]),
                op=ALU.mult,
            )

        neg_lam = keep.tile([P, 1], F32)

        def lam_value():
            lam_prod = keep.tile([P, 2, D], F32)
            nc.vector.tensor_tensor(out=lam_prod[:], in0=lam_vecs[:, 0:2, :], in1=lam_vecs[:, 2:4, :], op=ALU.mult)
            lam_dots = keep.tile([P, 2], F32)
            nc.vector.tensor_reduce(out=lam_dots[:], in_=lam_prod[:], axis=AXIS.X, op=ALU.add)
            lam_exps = keep.tile([P, 2], F32)
            nc.scalar.activation(out=lam_exps[:], in_=lam_dots[:], func=ACT.Exp)
            nc.vector.tensor_tensor(out=neg_lam[:], in0=lam_exps[:, 1:2], in1=lam_exps[:, 0:1], op=ALU.subtract)
            nc.vector.tensor_scalar_add(out=neg_lam[:], in0=neg_lam[:], scalar1=-LAM_INIT)

        LAG = 8

        def front(k):
            def live(lag):
                return 0 <= k - lag < BATCHES

            def second(lag):
                return live(lag) and (k - lag) % 2 == 1

            if live(2):
                find_max(k - 2)
                subtract_max(k - 2)
            if second(8):
                normalise(k - 8 - 1, 2 * BATCH)
            if second(6):
                invert(k - 6 - 1, 2 * BATCH)
            if second(5):
                add_up(k - 5 - 1, 2 * BATCH)
            if live(4):
                exponentials(k - 4)
                if k - 4 >= BATCHES - 3:
                    keep_clock(k - 4)

        def back(k):
            if 0 <= k < 14 and k % 2 == 1:
                scores(k - 1, 2)
            if 14 <= k < BATCHES:
                scores(k, 1)

        FIRST_TICK = FIRST_TICK_STEP
        for i in range(FIRST_TICK + BATCHES + LAG):
            k = i - FIRST_TICK
            if i < STEPS:
                new_y(i)
                project(i)
            if i in (5, 6):
                order_words(i - 3)
            if 0 <= i - 2 < STEPS:
                sort_rows(i - 2)
            front(k)
            if i < STEPS:
                split_hi(i, 0)
                split_lo(i, 0)
            if i in (6, 7):
                quantise(i - 4)
            if i < STEPS:
                split_hi(i, 1)
                split_lo(i, 1)
            if i < STEPS:
                back(k)
            if 0 <= i - 1 < STEPS:
                transpose_y(i - 1)
            if i >= STEPS:
                back(k)
            if i in (5, 6):
                transpose_x(i - 3)
            if i == 9:
                lam_value()

        plain = x_pool.tile([P, 4 * H, H], F32, tag="x_sb", align_bytes=256)
        result = x_pool.tile([P, 4 * H, H], F32, tag="grouped", align_bytes=256)
        for quad in range(H // 4):
            heads = slice(4 * quad, 4 * (quad + 1))
            for j in range(2):
                bank = psum.tile([P, BANK], F32, tag="bank")
                for slot in range(4):
                    column = 2 * (4 * quad + slot) + j
                    nc.tensor.transpose(bank[:, P * slot : P * (slot + 1)], w_all[:, column, :], ident[:])
                own = bank[:].rearrange("n (y a j) -> n a j y", y=4, j=2)[:, :, j, :]
                if j == 0:
                    nc.scalar.copy(out=plain[:, :, heads], in_=own)
                else:
                    nc.vector.scalar_tensor_tensor(
                        out=result[:, :, heads], in0=own, scalar=neg_lam[:, 0:1], in1=plain[:, :, heads],
                        op0=ALU.mult, op1=ALU.add,
                    )
        out_view = out.rearrange("(s w) (m u) a h -> s (w m) u (a h)", s=2, u=2)
        halves = result[:].rearrange("p (u s a) h -> p s u (a h)", u=2, s=2)
        for s in range(2):
            nc.sync.dma_start(out=out_view[s], in_=halves[:, s, :, :])
